import numpy as np
import ml_dtypes


def mxq(x, axis, fmt="e4m3"):
    dtype, down = {"e4m3": (ml_dtypes.float8_e4m3fn, 7), "e5m2": (ml_dtypes.float8_e5m2, 14)}[fmt]
    v = np.moveaxis(np.asarray(x, np.float32).astype(ml_dtypes.bfloat16).astype(np.float64), axis, -1)
    blocks = v.reshape(v.shape[:-1] + (-1, 32))
    amax = np.abs(blocks).max(-1, keepdims=True)
    byte = np.maximum(np.where(amax > 0, np.frexp(amax)[1] - 1 + 127, 0) - down, 1)
    scale = np.exp2(byte - 127.0)
    codes = (blocks / scale).astype(np.float32).astype(dtype).astype(np.float64)
    return np.moveaxis((codes * scale).reshape(v.shape), -1, axis)


WIDE = False


def mx_kscale(k):
    if not WIDE:
        return np.ones(k)
    levels = np.array([10, -10, 5, -5, 0])
    if k % 512:
        return np.exp2(np.random.permutation(np.resize(levels, k // 32))).repeat(32)
    a = np.empty((k // 512, 16))
    for p in range(k // 512):
        a[p, :8] = np.random.permutation(np.resize(levels, 8))
        for g in range(8):
            far = levels[np.abs(levels - a[p, g]) >= 10]
            a[p, g + 8] = far[np.random.randint(len(far))]
    return np.exp2(a.ravel()).repeat(32)


BF16 = ml_dtypes.bfloat16


def bf(x):
    return np.asarray(x, np.float32).astype(BF16)


def f64(x):
    return np.asarray(x).astype(np.float64)


E2M1 = np.array([0.0, 0.5, 1.0, 1.5, 2.0, 3.0, 4.0, 6.0, -0.0, -0.5, -1.0, -1.5, -2.0, -3.0, -4.0, -6.0])


def pack_weight(w, fmt):
    k, n = w.shape
    w = f64(bf(w)).reshape(k // 32, 32, n)
    amax = np.abs(w).max(1)
    if fmt == "e4m3":
        byte = np.frexp(amax)[1] - 1 + 127 - 7
    else:
        mant, ex = np.frexp(amax / 6.0)
        byte = np.where(mant > 0.5, ex, ex - 1) + 127
    byte = np.clip(np.where(amax > 0, byte, 1), 1, 254)
    scaled = (w * np.exp2(127.0 - byte)[:, None, :]).reshape(k, n).astype(np.float32)
    by_word = np.ascontiguousarray(scaled.reshape(k // 512, 128, 4, n).transpose(0, 1, 3, 2))
    if fmt == "e4m3":
        words = by_word.astype(ml_dtypes.float8_e4m3fn).view(np.uint8)
    else:
        c = by_word.astype(ml_dtypes.float4_e2m1fn).view(np.uint8) & 0xF
        words = c[..., 0::2] | (c[..., 1::2] << 4)
    return np.ascontiguousarray(words), np.ascontiguousarray(byte.astype(np.uint8).reshape(k // 512, 16, n))


def unpack_weight(words, scales, fmt):
    g, p, n, _ = words.shape
    if fmt == "e4m3":
        vals = np.ascontiguousarray(words).view(ml_dtypes.float8_e4m3fn).astype(np.float64)
    else:
        nib = np.empty((g, p, n, 4), np.uint8)
        nib[..., 0::2] = words & 0xF
        nib[..., 1::2] = words >> 4
        vals = E2M1[nib]
    vals = vals * np.repeat(np.exp2(scales.astype(np.float64) - 127.0), 8, axis=1)[..., None]
    return vals.transpose(0, 1, 3, 2).reshape(g * 512, n)
def pack4(w):
    words, scales = pack_weight(w, "e2m1")
    return words.reshape(words.shape[0], 128, -1), scales


def unpack4(words, scales):
    return unpack_weight(words.reshape(words.shape[0], 128, -1, 2), scales, "e2m1")


B, W, MID = 4096, 256, 1024


def draw0():
    s, t = mx_kscale(MID), mx_kscale(MID)
    h3 = bf(np.maximum(np.random.standard_normal((B, MID)), 0.0) * np.sqrt(2.0) * s)
    w4_words, w4_scales = pack4(np.random.standard_normal((MID, MID)) * np.sqrt(2.0 / MID) / s[:, None] * t)
    b4 = bf(np.random.standard_normal(MID) * 0.1 * t)
    w5_words, w5_scales = pack4(np.random.standard_normal((MID, W)) * 0.7 / np.sqrt(MID) / t[:, None])
    return {"h3": h3,
            "w4_words": w4_words,
            "w4_scales": w4_scales,
            "b4": b4,
            "w5_words": w5_words,
            "w5_scales": w5_scales,
            "b5": bf(np.random.standard_normal(W) * 0.2),
            "x": bf(np.random.standard_normal((B, W))),
            "log_det_J": bf(np.random.standard_normal(B) * 0.1 * np.sqrt(W))}


def core(h3, w4_words, w4_scales, b4, w5_words, w5_scales, b5, x, log_det_J):
    xf = f64(x)
    x1 = xf[:, 0::2]
    x2 = xf[:, 1::2]
    h4 = np.maximum((mxq(f64(h3), 1, "e4m3") @ unpack4(w4_words, w4_scales)) + f64(b4), 0.0)
    bvec = (mxq(h4, 1, "e4m3") @ unpack4(w5_words, w5_scales)) + f64(b5)
    b1t = np.tanh(bvec[:, 0::2])
    b2t = bvec[:, 1::2]
    y2 = x2 * np.exp(b1t) + b2t
    log_det = f64(log_det_J) + np.sum(b1t, axis=1)
    y = np.stack((x1, y2), axis=2).reshape(xf.shape)
    return (y, log_det)


def e4m3fn_bytes(y):
    return np.clip(np.asarray(y, np.float64), -448.0, 448.0).astype(np.float32).astype(ml_dtypes.float8_e4m3fn).view(np.uint8)


def e4m3fn_values(b):
    return np.asarray(b, np.uint8).view(ml_dtypes.float8_e4m3fn).astype(np.float64)


def setup_inputs():
    d = draw0()
    x0 = np.asarray(d['h3']).astype(np.float64)
    s = (np.max(np.abs(x0), axis=(0,), keepdims=True) / 448.0).astype(np.float32)
    out = {}
    for k, v in d.items():
        if k == 'h3':
            out['h3_bytes'] = e4m3fn_bytes(x0 / s.astype(np.float64))
            out['h3_scale'] = s
        else:
            out[k] = v
    return out


def reference(h3_bytes, h3_scale, w4_words, w4_scales, b4, w5_words, w5_scales, b5, x, log_det_J):
    return core(e4m3fn_values(h3_bytes) * h3_scale.astype(np.float64), w4_words, w4_scales, b4, w5_words, w5_scales, b5, x, log_det_J)

@@ -1,0 +1,350 @@
+from contextlib import ExitStack
+
+import concourse.mybir as mybir
+from concourse.masks import make_identity
+
+B, MID, W = 4096, 1024, 256
+FLOPS = 2 * B * MID * (MID + W)
+
+F32 = mybir.dt.float32
+BF16 = mybir.dt.bfloat16
+I32 = mybir.dt.int32
+U32 = mybir.dt.uint32
+U16 = mybir.dt.uint16
+U8 = mybir.dt.uint8
+FP8 = mybir.dt.float8_e4m3fn
+FP8X4 = mybir.dt.float8_e4m3fn_x4
+FP4X4 = mybir.dt.float4_e2m1fn_x4
+ALU = mybir.AluOpType
+ACT = mybir.ActivationFunctionType
+
+P = 128
+PACK = 4
+PASSES = MID // (P * PACK)
+TILES = B // P
+HALF = W // 2
+BANK = 512
+CHUNK_TILES = (2,) * 16
+
+
+def tile_affinecoupling_pa_t_w4_kernel(
+    tc, h3_bytes, h3_scale, w4_words, w4_scales, b4, w5_words, w5_scales, b5, x, log_det_j, out_0, out_1
+):
+    nc = tc.nc
+    chunks = len(CHUNK_TILES)
+    first = [sum(CHUNK_TILES[:c]) for c in range(chunks)]
+
+    with ExitStack() as ctx:
+        keep = ctx.enter_context(tc.tile_pool(name="keep", bufs=1))
+        work = ctx.enter_context(tc.tile_pool(name="work", bufs=2))
+        psum = ctx.enter_context(tc.psum_pool(name="psum", bufs=1))
+        ctx.enter_context(tc.manual_schedule())
+
+        h3_rows = h3_bytes.rearrange("(p j) k -> p j k", p=P)
+        x_rows = x.rearrange("(p j) w -> p j w", p=P)
+        y_rows = out_0.rearrange("(p j) w -> p j w", p=P)
+
+        ident_f32 = keep.tile([P, P], F32, name="ident_f32")
+        make_identity(nc, ident_f32[:])
+        ident_bf16 = keep.tile([P, P], BF16, name="ident_bf16")
+        make_identity(nc, ident_bf16[:])
+        ones = keep.tile([P, 1], F32, name="ones")
+        nc.gpsimd.memset(ones[:], 1.0)
+
+        w4s_raw = keep.tile([P, PASSES, MID], U8, name="w4s_raw")
+        w5s_raw = keep.tile([P, PASSES, W], U8, name="w5s_raw")
+        nc.vector.memset(w4s_raw[:].bitcast(I32), 0)
+        nc.vector.memset(w5s_raw[:].bitcast(I32), 0)
+
+        h3b = {}
+        xs = {}
+
+        def load_h3(c0, count):
+            tiles = sum(CHUNK_TILES[c0 : c0 + count])
+            h3_group = keep.tile([P, tiles, MID], U8, name="h3b%d" % c0)
+            nc.sync.dma_start(out=h3_group[:], in_=h3_rows[:, first[c0] : first[c0] + tiles, :])
+            for c in range(c0, c0 + count):
+                h3b[c] = h3_group[:, first[c] - first[c0] : first[c] - first[c0] + CHUNK_TILES[c], :]
+
+        def load_x(c0, count):
+            tiles = sum(CHUNK_TILES[c0 : c0 + count])
+            x_group = keep.tile([P, tiles, W], BF16, name="x%d" % c0)
+            nc.sync.dma_start(out=x_group[:], in_=x_rows[:, first[c0] : first[c0] + tiles, :])
+            for c in range(c0, c0 + count):
+                xs[c] = x_group[:, first[c] - first[c0] : first[c] - first[c0] + CHUNK_TILES[c], :]
+
+        def load_scale_rows(plane, scales):
+            for q in range(4):
+                nc.sync.dma_start(
+                    out=plane[32 * q : 32 * q + 4].bitcast(I32),
+                    in_=scales[:, 4 * q : 4 * q + 4, :].rearrange("g r n -> r g n").bitcast(I32),
+                )
+
+        scale_cols = keep.tile([P, 8], F32, name="scale_cols")
+        nc.sync.dma_start(out=scale_cols[:], in_=h3_scale.rearrange("o (p m) -> p (o m)", p=P))
+        load_h3(0, 1)
+        load_scale_rows(w4s_raw, w4_scales)
+        w4w_raw = keep.tile([P, PASSES, 2 * MID], U8, name="w4w_raw")
+        nc.sync.dma_start(out=w4w_raw[:].bitcast(I32), in_=w4_words.rearrange("g p n -> p g n").bitcast(I32))
+        load_h3(1, 1)
+        load_h3(2, 2)
+        b4_cols = keep.tile([P, PASSES * PACK], BF16, name="b4_cols")
+        nc.sync.dma_start(out=b4_cols[:].rearrange("p (g t) -> p g t", t=PACK), in_=b4.rearrange("(g p t) -> p g t", p=P, t=PACK))
+        load_scale_rows(w5s_raw, w5_scales)
+        w5w_raw = keep.tile([P, PASSES, 2 * W], U8, name="w5w_raw")
+        nc.sync.dma_start(out=w5w_raw[:].bitcast(I32), in_=w5_words.rearrange("g p n -> p g n").bitcast(I32))
+        load_h3(4, 2)
+        b5_cols = keep.tile([P, 2], BF16, name="b5_cols")
+        nc.sync.dma_start(out=b5_cols[:], in_=b5.rearrange("(p c) -> p c", p=P))
+        ldj = keep.tile([P, TILES], BF16, name="ldj")
+        nc.sync.dma_start(out=ldj[:], in_=log_det_j.rearrange("(p j) -> p j", p=P))
+        load_x(0, 4)
+        for c0 in range(6, chunks, 2):
+            load_h3(c0, min(2, chunks - c0))
+        for c0 in range(4, chunks, 4):
+            load_x(c0, min(4, chunks - c0))
+
+        scale_all = keep.tile([P, 2, MID // 2], F32, name="scale_all")
+        for u in range(2):
+            bank = psum.tile([P, 4, P], F32, tag="turn", bufs=2, name="spread")
+            for h in range(2):
+                for e in range(2):
+                    m = 4 * h + 2 * u + e
+                    nc.tensor.transpose(bank[:, 2 * h + e, :], scale_cols[:, m : m + 1].to_broadcast([P, P]), ident_f32[:])
+            spread = scale_all[:, u, :].rearrange("p (n s) -> p n s", s=4)
+            nc.scalar.activation(out=spread, in_=bank[:].rearrange("p s n -> p n s"), func=ACT.Copy)
+
+        w4w = keep.tile([P, PASSES, 2 * MID], U8, name="w4w", align_bytes=256)
+        w4s = keep.tile([P, PASSES, MID], U8, name="w4s", align_bytes=256)
+        w5w = keep.tile([P, PASSES, 2 * W], U8, name="w5w", align_bytes=256)
+        w5s = keep.tile([P, PASSES, W], U8, name="w5s", align_bytes=256)
+
+        def order_w4_words():
+            nc.scalar.copy(
+                out=w4w[:].bitcast(U16).rearrange("p g (a t m) -> p (g a) t m", t=PACK, m=P),
+                in_=w4w_raw[:].bitcast(U16).rearrange("p g (a m t) -> p (g a) t m", t=PACK, m=P),
+            )
+
+        def order_w4_scales():
+            nc.vector.tensor_copy(
+                out=w4s[:].rearrange("p g (a t m) -> p (g a) t m", t=PACK, m=P),
+                in_=w4s_raw[:].rearrange("p g (a m t) -> p (g a) t m", t=PACK, m=P),
+            )
+
+        def order_w5():
+            nc.scalar.copy(
+                out=w5w[:].bitcast(U16).rearrange("p g (c m) -> p g c m", c=2),
+                in_=w5w_raw[:].bitcast(U16).rearrange("p g (m c) -> p g c m", c=2),
+            )
+            nc.vector.tensor_copy(
+                out=w5s[:].rearrange("p g (c m) -> p g c m", c=2),
+                in_=w5s_raw[:].rearrange("p g (m c) -> p g c m", c=2),
+            )
+
+        log_det = keep.tile([P, TILES], F32, name="log_det")
+
+        wide = {}
+        turned = {}
+        h3q = {}
+        h4_planes = {}
+        h4_rows = {}
+        h4q = {}
+        ls = {}
+        scale_e = {}
+        side = {}
+        shift = {}
+        prod = {}
+        y2t = {}
+
+        def live(c, j=0):
+            return 0 <= c < chunks and j < CHUNK_TILES[c]
+
+        def widen(c, j):
+            if not live(c, j):
+                return
+            wide[c, j] = work.tile([P, MID], BF16, tag="wide", bufs=4, name="wide")
+            nc.vector.tensor_tensor(
+                out=wide[c, j][:].rearrange("p (u q e) -> p u q e", u=2, e=2),
+                in0=h3b[c][:, j, :].bitcast(FP8).rearrange("p (q u e) -> p u q e", u=2, e=2),
+                in1=scale_all[:].rearrange("p u (q e) -> p u q e", e=2),
+                op=ALU.mult,
+            )
+
+        def turn(c, j):
+            if not live(c, j):
+                return
+            n = CHUNK_TILES[c] * P
+            if j == 0:
+                turned[c] = work.tile([P, PASSES, n * PACK], BF16, tag="turned", name="turned", align_bytes=256)
+            words = wide[c, j][:].bitcast(F32)
+            bank = psum.tile([P, PASSES, 2, P], F32, tag="turn", bufs=2, name="turn")
+            for g in range(PASSES):
+                for u in range(2):
+                    at = (PASSES * u + g) * P
+                    nc.tensor.transpose(bank[:, g, u, :], words[:, at : at + P], ident_f32[:])
+            nc.scalar.copy(
+                out=turned[c][:].bitcast(F32)[:, :, 2 * P * j : 2 * P * (j + 1)].rearrange("p g (r u) -> p g r u", u=2),
+                in_=bank[:].rearrange("p g u r -> p g r u"),
+            )
+
+        def quantize(source, n, tag):
+            codes = work.tile([P, PASSES, n], U32, tag=tag + "_codes", bufs=3, name=tag + "_codes", align_bytes=256)
+            scales = work.tile([P, PASSES, n], U8, tag=tag + "_scales", bufs=3, name=tag + "_scales", align_bytes=256)
+            nc.vector.quantize_mx(
+                out=codes[:].rearrange("p g n -> p (g n)").bitcast(FP8X4),
+                scales=scales[:].rearrange("p g n -> p (g n)"),
+                in_=source[:].rearrange("p g n -> p (g n)"),
+            )
+            return codes, scales
+
+        def quantize_h3(c):
+            if live(c):
+                h3q[c] = quantize(turned[c], CHUNK_TILES[c] * P, "h3q")
+
+        def mx_product(acc, words, scales, col, operand, c):
+            for g in range(PASSES):
+                nc.tensor.matmul_mx(
+                    out=acc,
+                    lhsT=words[:, g, 2 * P * col : 2 * P * (col + 1)].bitcast(FP4X4),
+                    lhsT_scale=scales[:, g, P * col : P * (col + 1)],
+                    rhs=operand[c][0][:, g, :].bitcast(FP8X4),
+                    rhs_scale=operand[c][1][:, g, :],
+                    start=(g == 0),
+                    stop=(g == PASSES - 1),
+                )
+
+        def hidden(c, pair):
+            if not live(c):
+                return
+            n = CHUNK_TILES[c] * P
+            if pair == 0:
+                h4_planes[c] = work.tile([P, PASSES * PACK, n], BF16, tag="h4_planes", name="h4_planes")
+            acc = psum.tile([P, 2, n], F32, tag="acc", bufs=3, name="acc")
+            for i in range(2):
+                mx_product(acc[:, i, :], w4w, w4s, 2 * pair + i, h3q, c)
+            for i in range(2):
+                col = 2 * pair + i
+                nc.scalar.activation(out=h4_planes[c][:, col, :], in_=acc[:, i, :], func=ACT.Relu, bias=b4_cols[:, col : col + 1])
+
+        def interleave(c):
+            if not live(c):
+                return
+            n = CHUNK_TILES[c] * P
+            h4_rows[c] = work.tile([P, PASSES, n * PACK], BF16, tag="h4_rows", name="h4_rows", align_bytes=256)
+            nc.vector.tensor_copy(
+                out=h4_rows[c][:].rearrange("p g (r i t) -> p g r t i", i=4, t=PACK),
+                in_=h4_planes[c][:].rearrange("p (g t) (r i) -> p g r t i", i=4, t=PACK),
+            )
+
+        def quantize_h4(c):
+            if live(c):
+                h4q[c] = quantize(h4_rows[c], CHUNK_TILES[c] * P, "h4q")
+
+        def log_scale(c):
+            if not live(c):
+                return
+            n = CHUNK_TILES[c] * P
+            shift[c] = psum.tile([P, 2, n], F32, tag="v", name="v")
+            for half in range(2):
+                mx_product(shift[c][:, half, :], w5w, w5s, half, h4q, c)
+            ls[c] = work.tile([P, n], F32, tag="ls", name="ls")
+            nc.scalar.activation(out=ls[c][:], in_=shift[c][:, 0, :], func=ACT.Tanh, bias=b5_cols[:, 0:1])
+
+        def exp_scale(c):
+            if not live(c):
+                return
+            scale_e[c] = work.tile([P, CHUNK_TILES[c] * P], F32, tag="scale_e", name="scale_e")
+            nc.scalar.activation(out=scale_e[c][:], in_=ls[c][:], func=ACT.Exp)
+
+        def turn_x2_and_sum(c):
+            if not (live(c) or live(c - 1)):
+                return
+            side[c] = psum.tile([P, BANK], F32, tag="side", name="side")
+            for j in range(CHUNK_TILES[c] if live(c) else 0):
+                nc.tensor.transpose(side[c][:].bitcast(BF16)[:, P * j : P * (j + 1)], xs[c][:, j, 1::2], ident_bf16[:])
+            for j in range(CHUNK_TILES[c - 1] if live(c - 1) else 0):
+                nc.tensor.matmul(
+                    side[c][:, BANK // 2 + j : BANK // 2 + j + 1],
+                    lhsT=ls[c - 1][:, P * j : P * (j + 1)],
+                    rhs=ones[:],
+                    start=True,
+                    stop=True,
+                )
+
+        def product(c):
+            if not live(c):
+                return
+            n = CHUNK_TILES[c] * P
+            prod[c] = work.tile([P, n], F32, tag="prod", name="prod")
+            nc.vector.tensor_tensor(out=prod[c][:], in0=side[c][:].bitcast(BF16)[:, :n], in1=scale_e[c][:], op=ALU.mult)
+
+        def add_log_det(c):
+            if not live(c):
+                return
+            cols = slice(first[c], first[c] + CHUNK_TILES[c])
+            nc.vector.tensor_tensor(
+                out=log_det[:, cols],
+                in0=side[c + 1][:, BANK // 2 : BANK // 2 + CHUNK_TILES[c]],
+                in1=ldj[:, cols],
+                op=ALU.add,
+            )
+
+        def couple(c):
+            if not live(c):
+                return
+            y2t[c] = work.tile([P, CHUNK_TILES[c] * P], F32, tag="y2t", name="y2t")
+            nc.vector.scalar_tensor_tensor(
+                out=y2t[c][:], in0=shift[c][:, 1, :], scalar=b5_cols[:, 1:2], in1=prod[c][:], op0=ALU.add, op1=ALU.add
+            )
+
+        def finish(c):
+            if not live(c):
+                return
+            tiles = CHUNK_TILES[c]
+            bank = psum.tile([P, 2, tiles * HALF], F32, tag="y_bank", name="y_bank")
+            for j in range(tiles):
+                nc.tensor.transpose(bank[:, 1, HALF * j : HALF * (j + 1)], y2t[c][:, P * j : P * (j + 1)], ident_f32[:])
+            nc.tensor.matmul(
+                bank[:, 0, :],
+                lhsT=ident_bf16[:],
+                rhs=xs[c].rearrange("p j w -> p (j w)")[:, 0::2],
+                start=True,
+                stop=True,
+            )
+            y = work.tile([P, tiles, W], F32, tag="y", bufs=3, name="y")
+            nc.scalar.copy(out=y[:].rearrange("p j (m c) -> p (j m) c", c=2), in_=bank[:].rearrange("p c n -> p n c"))
+            nc.sync.dma_start(out=y_rows[:, first[c] : first[c] + tiles, :], in_=y[:])
+
+        order_w4_scales()
+        order_w4_words()
+        for c in range(2):
+            widen(c, 0)
+            widen(c, 1)
+            turn(c, 0)
+            turn(c, 1)
+        quantize_h3(0)
+        widen(2, 0)
+        widen(2, 1)
+        for step in range(chunks + 2):
+            interleave(step - 1)
+            widen(step + 3, 0)
+            if step == 1:
+                order_w5()
+            log_scale(step - 2)
+            hidden(step, 0)
+            exp_scale(step - 2)
+            for pair in range(1, 4):
+                hidden(step, pair)
+            product(step - 2)
+            add_log_det(step - 3)
+            quantize_h4(step - 1)
+            couple(step - 2)
+            turn(step + 2, 0)
+            turn(step + 2, 1)
+            turn_x2_and_sum(step - 1)
+            finish(step - 2)
+            widen(step + 3, 1)
+            quantize_h3(step + 1)
+        add_log_det(chunks - 1)
+
+        nc.sync.dma_start(out=out_1.rearrange("(p j) -> p j", p=P), in_=log_det[:])

@@ -25,6 +25,8 @@ TILES = B // P
 HALF = W // 2
 BANK = 512
 CHUNK_TILES = (2,) * 16
+TAIL = 1
+YTAIL = 3
 
 
 def tile_affinecoupling_pa_t_w4_kernel(
@@ -80,13 +82,17 @@ def tile_affinecoupling_pa_t_w4_kernel(
                     in_=scales[:, 4 * q : 4 * q + 4, :].rearrange("g r n -> r g n").bitcast(I32),
                 )
 
-        scale_cols = keep.tile([P, 8], F32, name="scale_cols")
-        nc.sync.dma_start(out=scale_cols[:], in_=h3_scale.rearrange("o (p m) -> p (o m)", p=P))
+        b5_raw = keep.tile([P, 2], BF16, name="b5_raw")
+        nc.sync.dma_start(out=b5_raw[:], in_=b5.rearrange("(p c) -> p c", p=P))
+        b5_cols = keep.tile([P, 2], F32, name="b5_cols")
+        nc.scalar.activation(out=b5_cols[:], in_=b5_raw[:], func=ACT.Copy)
         load_h3(0, 1)
-        load_scale_rows(w4s_raw, w4_scales)
+        scale_cols = keep.tile([P, PASSES, PACK], F32, name="scale_cols")
+        nc.sync.dma_start(out=scale_cols[:], in_=h3_scale.rearrange("o (g p t) -> p (o g) t", p=P, t=PACK))
         w4w_raw = keep.tile([P, PASSES, 2 * MID], U8, name="w4w_raw")
         nc.sync.dma_start(out=w4w_raw[:].bitcast(I32), in_=w4_words.rearrange("g p n -> p g n").bitcast(I32))
         load_h3(1, 1)
+        load_scale_rows(w4s_raw, w4_scales)
         load_h3(2, 2)
         b4_cols = keep.tile([P, PASSES * PACK], BF16, name="b4_cols")
         nc.sync.dma_start(out=b4_cols[:].rearrange("p (g t) -> p g t", t=PACK), in_=b4.rearrange("(g p t) -> p g t", p=P, t=PACK))
@@ -94,8 +100,6 @@ def tile_affinecoupling_pa_t_w4_kernel(
         w5w_raw = keep.tile([P, PASSES, 2 * W], U8, name="w5w_raw")
         nc.sync.dma_start(out=w5w_raw[:].bitcast(I32), in_=w5_words.rearrange("g p n -> p g n").bitcast(I32))
         load_h3(4, 2)
-        b5_cols = keep.tile([P, 2], BF16, name="b5_cols")
-        nc.sync.dma_start(out=b5_cols[:], in_=b5.rearrange("(p c) -> p c", p=P))
         ldj = keep.tile([P, TILES], BF16, name="ldj")
         nc.sync.dma_start(out=ldj[:], in_=log_det_j.rearrange("(p j) -> p j", p=P))
         load_x(0, 4)
@@ -104,31 +108,23 @@ def tile_affinecoupling_pa_t_w4_kernel(
         for c0 in range(4, chunks, 4):
             load_x(c0, min(4, chunks - c0))
 
-        scale_all = keep.tile([P, 2, MID // 2], F32, name="scale_all")
-        for u in range(2):
-            bank = psum.tile([P, 4, P], F32, tag="turn", bufs=2, name="spread")
-            for h in range(2):
-                for e in range(2):
-                    m = 4 * h + 2 * u + e
-                    nc.tensor.transpose(bank[:, 2 * h + e, :], scale_cols[:, m : m + 1].to_broadcast([P, P]), ident_f32[:])
-            spread = scale_all[:, u, :].rearrange("p (n s) -> p n s", s=4)
-            nc.scalar.activation(out=spread, in_=bank[:].rearrange("p s n -> p n s"), func=ACT.Copy)
-
         w4w = keep.tile([P, PASSES, 2 * MID], U8, name="w4w", align_bytes=256)
         w4s = keep.tile([P, PASSES, MID], U8, name="w4s", align_bytes=256)
         w5w = keep.tile([P, PASSES, 2 * W], U8, name="w5w", align_bytes=256)
         w5s = keep.tile([P, PASSES, W], U8, name="w5s", align_bytes=256)
 
-        def order_w4_words():
+        def order_w4_words(a):
+            cols = slice(MID // 2 * a, MID // 2 * (a + 1))
             nc.scalar.copy(
-                out=w4w[:].bitcast(U16).rearrange("p g (a t m) -> p (g a) t m", t=PACK, m=P),
-                in_=w4w_raw[:].bitcast(U16).rearrange("p g (a m t) -> p (g a) t m", t=PACK, m=P),
+                out=w4w[:].bitcast(U16)[:, :, cols].rearrange("p g (t m) -> p g t m", t=PACK),
+                in_=w4w_raw[:].bitcast(U16)[:, :, cols].rearrange("p g (m t) -> p g t m", t=PACK),
             )
 
-        def order_w4_scales():
+        def order_w4_scales(a):
+            cols = slice(MID // 2 * a, MID // 2 * (a + 1))
             nc.vector.tensor_copy(
-                out=w4s[:].rearrange("p g (a t m) -> p (g a) t m", t=PACK, m=P),
-                in_=w4s_raw[:].rearrange("p g (a m t) -> p (g a) t m", t=PACK, m=P),
+                out=w4s[:, :, cols].rearrange("p g (t m) -> p g t m", t=PACK),
+                in_=w4s_raw[:, :, cols].rearrange("p g (m t) -> p g t m", t=PACK),
             )
 
         def order_w5():
@@ -145,6 +141,8 @@ def tile_affinecoupling_pa_t_w4_kernel(
 
         wide = {}
         turned = {}
+        turn_bank = {}
+        y_bank = {}
         h3q = {}
         h4_planes = {}
         h4_rows = {}
@@ -163,28 +161,32 @@ def tile_affinecoupling_pa_t_w4_kernel(
             if not live(c, j):
                 return
             wide[c, j] = work.tile([P, MID], BF16, tag="wide", bufs=4, name="wide")
-            nc.vector.tensor_tensor(
+            nc.scalar.copy(
                 out=wide[c, j][:].rearrange("p (u q e) -> p u q e", u=2, e=2),
-                in0=h3b[c][:, j, :].bitcast(FP8).rearrange("p (q u e) -> p u q e", u=2, e=2),
-                in1=scale_all[:].rearrange("p u (q e) -> p u q e", e=2),
-                op=ALU.mult,
+                in_=h3b[c][:, j, :].bitcast(FP8).rearrange("p (q u e) -> p u q e", u=2, e=2),
             )
 
         def turn(c, j):
             if not live(c, j):
                 return
-            n = CHUNK_TILES[c] * P
-            if j == 0:
-                turned[c] = work.tile([P, PASSES, n * PACK], BF16, tag="turned", name="turned", align_bytes=256)
             words = wide[c, j][:].bitcast(F32)
-            bank = psum.tile([P, PASSES, 2, P], F32, tag="turn", bufs=2, name="turn")
-            for g in range(PASSES):
-                for u in range(2):
+            turn_bank[c, j] = psum.tile([P, 2, PASSES, P], F32, tag="turn", bufs=2, name="turn")
+            for u in range(2):
+                for g in range(PASSES):
                     at = (PASSES * u + g) * P
-                    nc.tensor.transpose(bank[:, g, u, :], words[:, at : at + P], ident_f32[:])
-            nc.scalar.copy(
-                out=turned[c][:].bitcast(F32)[:, :, 2 * P * j : 2 * P * (j + 1)].rearrange("p g (r u) -> p g r u", u=2),
-                in_=bank[:].rearrange("p g u r -> p g r u"),
+                    nc.tensor.transpose(turn_bank[c, j][:, u, g, :], words[:, at : at + P], ident_f32[:])
+
+        def apply_scale(c, j):
+            if not live(c, j):
+                return
+            if j == 0:
+                n = CHUNK_TILES[c] * P
+                turned[c] = work.tile([P, PASSES, n * PACK], BF16, tag="turned", name="turned", align_bytes=256)
+            nc.vector.tensor_tensor(
+                out=turned[c][:, :, PACK * P * j : PACK * P * (j + 1)].rearrange("p g (r u e) -> p g r u e", u=2, e=2),
+                in0=turn_bank[c, j][:].bitcast(BF16).rearrange("p u g (r e) -> p g r u e", e=2),
+                in1=scale_cols[:].rearrange("p g (u e) -> p g u e", e=2).unsqueeze(2).to_broadcast([P, PASSES, P, 2, 2]),
+                op=ALU.mult,
             )
 
         def quantize(source, n, tag):
@@ -230,11 +232,21 @@ def tile_affinecoupling_pa_t_w4_kernel(
             if not live(c):
                 return
             n = CHUNK_TILES[c] * P
-            h4_rows[c] = work.tile([P, PASSES, n * PACK], BF16, tag="h4_rows", name="h4_rows", align_bytes=256)
-            nc.vector.tensor_copy(
-                out=h4_rows[c][:].rearrange("p g (r i t) -> p g r t i", i=4, t=PACK),
-                in_=h4_planes[c][:].rearrange("p (g t) (r i) -> p g r t i", i=4, t=PACK),
-            )
+            h4_rows[c] = work.tile([P, PASSES, n * PACK], BF16, tag="h4_rows", bufs=1, name="h4_rows", align_bytes=256)
+            if c < chunks - TAIL:
+                nc.gpsimd.tensor_scalar(
+                    out=h4_rows[c][:].rearrange("p g (r t) -> p g r t", t=PACK),
+                    in0=h4_planes[c][:].rearrange("p (g t) r -> p g r t", t=PACK),
+                    scalar1=1.0,
+                    scalar2=0.0,
+                    op0=ALU.mult,
+                    op1=ALU.add,
+                )
+            else:
+                nc.vector.tensor_copy(
+                    out=h4_rows[c][:].rearrange("p g (r i t) -> p g r t i", i=4, t=PACK),
+                    in_=h4_planes[c][:].rearrange("p (g t) (r i) -> p g r t i", i=4, t=PACK),
+                )
 
         def quantize_h4(c):
             if live(c):
@@ -297,37 +309,53 @@ def tile_affinecoupling_pa_t_w4_kernel(
                 out=y2t[c][:], in0=shift[c][:, 1, :], scalar=b5_cols[:, 1:2], in1=prod[c][:], op0=ALU.add, op1=ALU.add
             )
 
-        def finish(c):
+        def turn_y(c):
             if not live(c):
                 return
             tiles = CHUNK_TILES[c]
-            bank = psum.tile([P, 2, tiles * HALF], F32, tag="y_bank", name="y_bank")
+            y_bank[c] = psum.tile([P, 2, tiles * HALF], F32, tag="y_bank", name="y_bank")
             for j in range(tiles):
-                nc.tensor.transpose(bank[:, 1, HALF * j : HALF * (j + 1)], y2t[c][:, P * j : P * (j + 1)], ident_f32[:])
+                nc.tensor.transpose(y_bank[c][:, 1, HALF * j : HALF * (j + 1)], y2t[c][:, P * j : P * (j + 1)], ident_f32[:])
             nc.tensor.matmul(
-                bank[:, 0, :],
+                y_bank[c][:, 0, :],
                 lhsT=ident_bf16[:],
                 rhs=xs[c].rearrange("p j w -> p (j w)")[:, 0::2],
                 start=True,
                 stop=True,
             )
+
+        def store_y(c):
+            if not live(c):
+                return
+            tiles = CHUNK_TILES[c]
             y = work.tile([P, tiles, W], F32, tag="y", bufs=3, name="y")
-            nc.scalar.copy(out=y[:].rearrange("p j (m c) -> p (j m) c", c=2), in_=bank[:].rearrange("p c n -> p n c"))
+            copy_out = nc.vector.tensor_copy if c < chunks - YTAIL else nc.scalar.copy
+            copy_out(
+                out=y[:].rearrange("p j (m c) -> p (j m) c", c=2), in_=y_bank[c][:].rearrange("p c n -> p n c")
+            )
             nc.sync.dma_start(out=y_rows[:, first[c] : first[c] + tiles, :], in_=y[:])
 
-        order_w4_scales()
-        order_w4_words()
-        for c in range(2):
-            widen(c, 0)
-            widen(c, 1)
-            turn(c, 0)
-            turn(c, 1)
+        widen(0, 0)
+        widen(0, 1)
+        turn(0, 0)
+        turn(0, 1)
+        order_w4_words(0)
+        widen(1, 0)
+        widen(1, 1)
+        apply_scale(0, 0)
+        apply_scale(0, 1)
+        order_w4_scales(0)
         quantize_h3(0)
+        order_w4_scales(1)
+        order_w4_words(1)
+        turn(1, 0)
+        turn(1, 1)
         widen(2, 0)
         widen(2, 1)
-        for step in range(chunks + 2):
-            interleave(step - 1)
-            widen(step + 3, 0)
+        for step in range(chunks + 3):
+            apply_scale(step + 1, 0)
+            apply_scale(step + 1, 1)
+            store_y(step - 3)
             if step == 1:
                 order_w5()
             log_scale(step - 2)
@@ -337,14 +365,15 @@ def tile_affinecoupling_pa_t_w4_kernel(
                 hidden(step, pair)
             product(step - 2)
             add_log_det(step - 3)
-            quantize_h4(step - 1)
             couple(step - 2)
+            quantize_h4(step - 1)
+            quantize_h3(step + 1)
+            interleave(step)
             turn(step + 2, 0)
             turn(step + 2, 1)
             turn_x2_and_sum(step - 1)
-            finish(step - 2)
+            turn_y(step - 2)
+            widen(step + 3, 0)
             widen(step + 3, 1)
-            quantize_h3(step + 1)
-        add_log_det(chunks - 1)
 
         nc.sync.dma_start(out=out_1.rearrange("(p j) -> p j", p=P), in_=log_det[:])

@@ -25,8 +25,9 @@ TILES = B // P
 HALF = W // 2
 BANK = 512
 CHUNK_TILES = (2,) * 16
-TAIL = 1
-YTAIL = 3
+ALL, FIRST, SECOND = slice(0, PASSES), slice(0, 1), slice(1, 2)
+BANK_BUFS = {"turn": 2, "acc": 3, "v": 1, "y": 1}
+X2_AT = (0, 256, 768)
 
 
 def tile_affinecoupling_pa_t_w4_kernel(
@@ -61,12 +62,11 @@ def tile_affinecoupling_pa_t_w4_kernel(
         h3b = {}
         xs = {}
 
-        def load_h3(c0, count):
-            tiles = sum(CHUNK_TILES[c0 : c0 + count])
-            h3_group = keep.tile([P, tiles, MID], U8, name="h3b%d" % c0)
-            nc.sync.dma_start(out=h3_group[:], in_=h3_rows[:, first[c0] : first[c0] + tiles, :])
-            for c in range(c0, c0 + count):
-                h3b[c] = h3_group[:, first[c] - first[c0] : first[c] - first[c0] + CHUNK_TILES[c], :]
+        def load_h3(j0, tiles):
+            h3_group = keep.tile([P, tiles, MID], U8, name="h3b%d" % j0)
+            nc.sync.dma_start(out=h3_group[:], in_=h3_rows[:, j0 : j0 + tiles, :])
+            for j in range(tiles):
+                h3b[j0 + j] = h3_group[:, j, :]
 
         def load_x(c0, count):
             tiles = sum(CHUNK_TILES[c0 : c0 + count])
@@ -87,24 +87,25 @@ def tile_affinecoupling_pa_t_w4_kernel(
         b5_cols = keep.tile([P, 2], F32, name="b5_cols")
         nc.scalar.activation(out=b5_cols[:], in_=b5_raw[:], func=ACT.Copy)
         load_h3(0, 1)
+        load_h3(1, 1)
         scale_cols = keep.tile([P, PASSES, PACK], F32, name="scale_cols")
         nc.sync.dma_start(out=scale_cols[:], in_=h3_scale.rearrange("o (g p t) -> p (o g) t", p=P, t=PACK))
         w4w_raw = keep.tile([P, PASSES, 2 * MID], U8, name="w4w_raw")
         nc.sync.dma_start(out=w4w_raw[:].bitcast(I32), in_=w4_words.rearrange("g p n -> p g n").bitcast(I32))
-        load_h3(1, 1)
-        load_scale_rows(w4s_raw, w4_scales)
         load_h3(2, 2)
+        load_scale_rows(w4s_raw, w4_scales)
+        load_h3(4, 4)
         b4_cols = keep.tile([P, PASSES * PACK], BF16, name="b4_cols")
         nc.sync.dma_start(out=b4_cols[:].rearrange("p (g t) -> p g t", t=PACK), in_=b4.rearrange("(g p t) -> p g t", p=P, t=PACK))
         load_scale_rows(w5s_raw, w5_scales)
         w5w_raw = keep.tile([P, PASSES, 2 * W], U8, name="w5w_raw")
         nc.sync.dma_start(out=w5w_raw[:].bitcast(I32), in_=w5_words.rearrange("g p n -> p g n").bitcast(I32))
-        load_h3(4, 2)
+        load_h3(8, 4)
         ldj = keep.tile([P, TILES], BF16, name="ldj")
         nc.sync.dma_start(out=ldj[:], in_=log_det_j.rearrange("(p j) -> p j", p=P))
         load_x(0, 4)
-        for c0 in range(6, chunks, 2):
-            load_h3(c0, min(2, chunks - c0))
+        for j0 in range(12, TILES, 4):
+            load_h3(j0, 4)
         for c0 in range(4, chunks, 4):
             load_x(c0, min(4, chunks - c0))
 
@@ -127,11 +128,13 @@ def tile_affinecoupling_pa_t_w4_kernel(
                 in_=w4s_raw[:, :, cols].rearrange("p g (m t) -> p g t m", t=PACK),
             )
 
-        def order_w5():
+        def order_w5_words():
             nc.scalar.copy(
                 out=w5w[:].bitcast(U16).rearrange("p g (c m) -> p g c m", c=2),
                 in_=w5w_raw[:].bitcast(U16).rearrange("p g (m c) -> p g c m", c=2),
             )
+
+        def order_w5_scales():
             nc.vector.tensor_copy(
                 out=w5s[:].rearrange("p g (c m) -> p g c m", c=2),
                 in_=w5s_raw[:].rearrange("p g (m c) -> p g c m", c=2),
@@ -149,8 +152,9 @@ def tile_affinecoupling_pa_t_w4_kernel(
         h4q = {}
         ls = {}
         scale_e = {}
-        side = {}
-        shift = {}
+        side = psum.tile([P, BANK], F32, name="side")
+        v_even = {}
+        v_odd = {}
         prod = {}
         y2t = {}
 
@@ -163,7 +167,7 @@ def tile_affinecoupling_pa_t_w4_kernel(
             wide[c, j] = work.tile([P, MID], BF16, tag="wide", bufs=4, name="wide")
             nc.scalar.copy(
                 out=wide[c, j][:].rearrange("p (u q e) -> p u q e", u=2, e=2),
-                in_=h3b[c][:, j, :].bitcast(FP8).rearrange("p (q u e) -> p u q e", u=2, e=2),
+                in_=h3b[first[c] + j].bitcast(FP8).rearrange("p (q u e) -> p u q e", u=2, e=2),
             )
 
         def turn(c, j):
@@ -189,19 +193,21 @@ def tile_affinecoupling_pa_t_w4_kernel(
                 op=ALU.mult,
             )
 
-        def quantize(source, n, tag):
-            codes = work.tile([P, PASSES, n], U32, tag=tag + "_codes", bufs=3, name=tag + "_codes", align_bytes=256)
-            scales = work.tile([P, PASSES, n], U8, tag=tag + "_scales", bufs=3, name=tag + "_scales", align_bytes=256)
+        def quantize(store, c, source, tag, passes):
+            n = CHUNK_TILES[c] * P
+            if passes.start == 0:
+                codes = work.tile([P, PASSES, n], U32, tag=tag + "_codes", bufs=3, name=tag + "_codes", align_bytes=256)
+                scales = work.tile([P, PASSES, n], U8, tag=tag + "_scales", bufs=3, name=tag + "_scales", align_bytes=256)
+                store[c] = codes, scales
             nc.vector.quantize_mx(
-                out=codes[:].rearrange("p g n -> p (g n)").bitcast(FP8X4),
-                scales=scales[:].rearrange("p g n -> p (g n)"),
-                in_=source[:].rearrange("p g n -> p (g n)"),
+                out=store[c][0][:, passes, :].rearrange("p g n -> p (g n)").bitcast(FP8X4),
+                scales=store[c][1][:, passes, :].rearrange("p g n -> p (g n)"),
+                in_=source[:, passes, :].rearrange("p g n -> p (g n)"),
             )
-            return codes, scales
 
         def quantize_h3(c):
             if live(c):
-                h3q[c] = quantize(turned[c], CHUNK_TILES[c] * P, "h3q")
+                quantize(h3q, c, turned[c], "h3q", ALL)
 
         def mx_product(acc, words, scales, col, operand, c):
             for g in range(PASSES):
@@ -228,39 +234,52 @@ def tile_affinecoupling_pa_t_w4_kernel(
                 col = 2 * pair + i
                 nc.scalar.activation(out=h4_planes[c][:, col, :], in_=acc[:, i, :], func=ACT.Relu, bias=b4_cols[:, col : col + 1])
 
-        def interleave(c):
-            if not live(c):
-                return
+        def new_rows(c, tag):
             n = CHUNK_TILES[c] * P
-            h4_rows[c] = work.tile([P, PASSES, n * PACK], BF16, tag="h4_rows", bufs=1, name="h4_rows", align_bytes=256)
-            if c < chunks - TAIL:
-                nc.gpsimd.tensor_scalar(
-                    out=h4_rows[c][:].rearrange("p g (r t) -> p g r t", t=PACK),
-                    in0=h4_planes[c][:].rearrange("p (g t) r -> p g r t", t=PACK),
-                    scalar1=1.0,
-                    scalar2=0.0,
-                    op0=ALU.mult,
-                    op1=ALU.add,
-                )
-            else:
-                nc.vector.tensor_copy(
-                    out=h4_rows[c][:].rearrange("p g (r i t) -> p g r t i", i=4, t=PACK),
-                    in_=h4_planes[c][:].rearrange("p (g t) (r i) -> p g r t i", i=4, t=PACK),
-                )
+            h4_rows[c] = work.tile([P, PASSES, n * PACK], BF16, tag=tag, bufs=1, name="h4_rows", align_bytes=256)
 
-        def quantize_h4(c):
+        def interleave_gpsimd(c, passes):
+            nc.gpsimd.tensor_scalar(
+                out=h4_rows[c][:, passes, :].rearrange("p g (r t) -> p g r t", t=PACK),
+                in0=h4_planes[c][:].rearrange("p (g t) r -> p g r t", t=PACK)[:, passes],
+                scalar1=1.0,
+                scalar2=0.0,
+                op0=ALU.mult,
+                op1=ALU.add,
+            )
+
+        def interleave_vector(c, passes):
+            nc.vector.tensor_copy(
+                out=h4_rows[c][:, passes, :].rearrange("p g (r i t) -> p g r t i", i=4, t=PACK),
+                in_=h4_planes[c][:].rearrange("p (g t) (r i) -> p g r t i", i=4, t=PACK)[:, passes],
+            )
+
+        def quantize_h4(c, passes):
             if live(c):
-                h4q[c] = quantize(h4_rows[c], CHUNK_TILES[c] * P, "h4q")
+                quantize(h4q, c, h4_rows[c], "h4q", passes)
 
-        def log_scale(c):
+        def log_scale(c, tag="v"):
             if not live(c):
                 return
             n = CHUNK_TILES[c] * P
-            shift[c] = psum.tile([P, 2, n], F32, tag="v", name="v")
-            for half in range(2):
-                mx_product(shift[c][:, half, :], w5w, w5s, half, h4q, c)
-            ls[c] = work.tile([P, n], F32, tag="ls", name="ls")
-            nc.scalar.activation(out=ls[c][:], in_=shift[c][:, 0, :], func=ACT.Tanh, bias=b5_cols[:, 0:1])
+            bank = psum.tile([P, 2, n], F32, tag=tag, bufs=BANK_BUFS[tag], name="v")
+            v_even[c], v_odd[c] = bank[:, 0, :], bank[:, 1, :]
+            mx_product(v_even[c], w5w, w5s, 0, h4q, c)
+            mx_product(v_odd[c], w5w, w5s, 1, h4q, c)
+
+        def log_scale_apart(c):
+            n = CHUNK_TILES[c] * P
+            even_bank = psum.tile([P, n], F32, tag="v", bufs=BANK_BUFS["v"], name="v_even")
+            odd_bank = psum.tile([P, n], F32, tag="acc", bufs=BANK_BUFS["acc"], name="v_odd")
+            v_even[c], v_odd[c] = even_bank[:], odd_bank[:]
+            mx_product(v_even[c], w5w, w5s, 0, h4q, c)
+            mx_product(v_odd[c], w5w, w5s, 1, h4q, c)
+
+        def tanh_scale(c):
+            if not live(c):
+                return
+            ls[c] = work.tile([P, CHUNK_TILES[c] * P], F32, tag="ls", bufs=3, name="ls")
+            nc.scalar.activation(out=ls[c][:], in_=v_even[c], func=ACT.Tanh, bias=b5_cols[:, 0:1])
 
         def exp_scale(c):
             if not live(c):
@@ -268,72 +287,66 @@ def tile_affinecoupling_pa_t_w4_kernel(
             scale_e[c] = work.tile([P, CHUNK_TILES[c] * P], F32, tag="scale_e", name="scale_e")
             nc.scalar.activation(out=scale_e[c][:], in_=ls[c][:], func=ACT.Exp)
 
-        def turn_x2_and_sum(c):
-            if not (live(c) or live(c - 1)):
+        def turn_x2(c):
+            if not live(c):
                 return
-            side[c] = psum.tile([P, BANK], F32, tag="side", name="side")
-            for j in range(CHUNK_TILES[c] if live(c) else 0):
-                nc.tensor.transpose(side[c][:].bitcast(BF16)[:, P * j : P * (j + 1)], xs[c][:, j, 1::2], ident_bf16[:])
-            for j in range(CHUNK_TILES[c - 1] if live(c - 1) else 0):
-                nc.tensor.matmul(
-                    side[c][:, BANK // 2 + j : BANK // 2 + j + 1],
-                    lhsT=ls[c - 1][:, P * j : P * (j + 1)],
-                    rhs=ones[:],
-                    start=True,
-                    stop=True,
-                )
+            for j in range(CHUNK_TILES[c]):
+                at = X2_AT[c % 3] + P * j
+                nc.tensor.transpose(side[:].bitcast(BF16)[:, at : at + P], xs[c][:, j, 1::2], ident_bf16[:])
+
+        def sum_ls(c):
+            if not live(c):
+                return
+            for j in range(CHUNK_TILES[c]):
+                at = BANK // 2 + first[c] + j
+                nc.tensor.matmul(side[:, at : at + 1], lhsT=ls[c][:, P * j : P * (j + 1)], rhs=ones[:], start=True, stop=True)
 
         def product(c):
             if not live(c):
                 return
             n = CHUNK_TILES[c] * P
             prod[c] = work.tile([P, n], F32, tag="prod", name="prod")
-            nc.vector.tensor_tensor(out=prod[c][:], in0=side[c][:].bitcast(BF16)[:, :n], in1=scale_e[c][:], op=ALU.mult)
-
-        def add_log_det(c):
-            if not live(c):
-                return
-            cols = slice(first[c], first[c] + CHUNK_TILES[c])
-            nc.vector.tensor_tensor(
-                out=log_det[:, cols],
-                in0=side[c + 1][:, BANK // 2 : BANK // 2 + CHUNK_TILES[c]],
-                in1=ldj[:, cols],
-                op=ALU.add,
-            )
+            nc.vector.tensor_tensor(out=prod[c][:], in0=side[:].bitcast(BF16)[:, X2_AT[c % 3] : X2_AT[c % 3] + n], in1=scale_e[c][:], op=ALU.mult)
 
         def couple(c):
             if not live(c):
                 return
             y2t[c] = work.tile([P, CHUNK_TILES[c] * P], F32, tag="y2t", name="y2t")
             nc.vector.scalar_tensor_tensor(
-                out=y2t[c][:], in0=shift[c][:, 1, :], scalar=b5_cols[:, 1:2], in1=prod[c][:], op0=ALU.add, op1=ALU.add
+                out=y2t[c][:], in0=v_odd[c], scalar=b5_cols[:, 1:2], in1=prod[c][:], op0=ALU.add, op1=ALU.add
             )
 
-        def turn_y(c):
+        def turn_y(c, tag="y", part=slice(0, 2)):
             if not live(c):
                 return
-            tiles = CHUNK_TILES[c]
-            y_bank[c] = psum.tile([P, 2, tiles * HALF], F32, tag="y_bank", name="y_bank")
-            for j in range(tiles):
-                nc.tensor.transpose(y_bank[c][:, 1, HALF * j : HALF * (j + 1)], y2t[c][:, P * j : P * (j + 1)], ident_f32[:])
+            tiles = part.stop - part.start
+            bank = psum.tile([P, 2, tiles * HALF], F32, tag=tag, bufs=BANK_BUFS[tag], name="y_bank")
+            y_bank[c, part.start] = bank
             nc.tensor.matmul(
-                y_bank[c][:, 0, :],
+                bank[:, 0, :],
                 lhsT=ident_bf16[:],
-                rhs=xs[c].rearrange("p j w -> p (j w)")[:, 0::2],
+                rhs=xs[c][:, part, :].rearrange("p j w -> p (j w)")[:, 0::2],
                 start=True,
                 stop=True,
             )
+            for j in range(tiles):
+                at = P * (part.start + j)
+                nc.tensor.transpose(bank[:, 1, HALF * j : HALF * (j + 1)], y2t[c][:, at : at + P], ident_f32[:])
 
-        def store_y(c):
+        def store_y(c, copy_out, part=slice(0, 2)):
             if not live(c):
                 return
-            tiles = CHUNK_TILES[c]
-            y = work.tile([P, tiles, W], F32, tag="y", bufs=3, name="y")
-            copy_out = nc.vector.tensor_copy if c < chunks - YTAIL else nc.scalar.copy
+            tiles = part.stop - part.start
+            y = work.tile([P, tiles, W], F32, tag="y", bufs=5, name="y")
             copy_out(
-                out=y[:].rearrange("p j (m c) -> p (j m) c", c=2), in_=y_bank[c][:].rearrange("p c n -> p n c")
+                out=y[:].rearrange("p j (m c) -> p (j m) c", c=2),
+                in_=y_bank[c, part.start][:].rearrange("p c n -> p n c"),
             )
-            nc.sync.dma_start(out=y_rows[:, first[c] : first[c] + tiles, :], in_=y[:])
+            nc.sync.dma_start(out=y_rows[:, first[c] + part.start : first[c] + part.stop, :], in_=y[:])
+
+        def store_log_det():
+            nc.vector.tensor_tensor(out=log_det[:], in0=side[:, BANK // 2 : BANK // 2 + TILES], in1=ldj[:], op=ALU.add)
+            nc.sync.dma_start(out=out_1.rearrange("(p j) -> p j", p=P), in_=log_det[:])
 
         widen(0, 0)
         widen(0, 1)
@@ -352,28 +365,90 @@ def tile_affinecoupling_pa_t_w4_kernel(
         turn(1, 1)
         widen(2, 0)
         widen(2, 1)
-        for step in range(chunks + 3):
+        for step in range(chunks - 2):
             apply_scale(step + 1, 0)
+            product(step - 3)
+            store_y(step - 4, nc.vector.tensor_copy)
+            couple(step - 3)
             apply_scale(step + 1, 1)
-            store_y(step - 3)
-            if step == 1:
-                order_w5()
-            log_scale(step - 2)
-            hidden(step, 0)
-            exp_scale(step - 2)
-            for pair in range(1, 4):
+            if step == 0:
+                order_w5_scales()
+            for pair in range(4):
                 hidden(step, pair)
-            product(step - 2)
-            add_log_det(step - 3)
-            couple(step - 2)
-            quantize_h4(step - 1)
+            log_scale(step - 2)
+            tanh_scale(step - 2)
+            quantize_h4(step - 1, ALL)
             quantize_h3(step + 1)
-            interleave(step)
+            new_rows(step, "rows")
+            interleave_gpsimd(step, ALL)
             turn(step + 2, 0)
             turn(step + 2, 1)
-            turn_x2_and_sum(step - 1)
-            turn_y(step - 2)
+            turn_x2(step - 2)
+            sum_ls(step - 3)
+            turn_y(step - 3)
             widen(step + 3, 0)
+            exp_scale(step - 2)
             widen(step + 3, 1)
-
-        nc.sync.dma_start(out=out_1.rearrange("(p j) -> p j", p=P), in_=log_det[:])
+            if step == 1:
+                order_w5_words()
+        z = chunks - 1
+        apply_scale(z, 0)
+        product(z - 4)
+        store_y(z - 5, nc.scalar.copy)
+        apply_scale(z, 1)
+        couple(z - 4)
+        for pair in range(4):
+            hidden(z - 1, pair)
+        log_scale(z - 3)
+        tanh_scale(z - 3)
+        quantize_h3(z)
+        quantize_h4(z - 2, ALL)
+        turn_x2(z - 3)
+        sum_ls(z - 4)
+        turn_y(z - 4)
+        exp_scale(z - 3)
+        store_y(z - 4, nc.scalar.copy)
+        new_rows(z - 1, "rows_a")
+        interleave_vector(z - 1, ALL)
+        for pair in range(4):
+            hidden(z, pair)
+        product(z - 3)
+        quantize_h4(z - 1, ALL)
+        couple(z - 3)
+        new_rows(z, "rows_b")
+        interleave_vector(z, FIRST)
+        log_scale(z - 2, "turn")
+        log_scale(z - 1, "turn")
+        for c in range(z - 2, z + 1):
+            turn_x2(c)
+        sum_ls(z - 3)
+        turn_y(z - 3)
+        quantize_h4(z, FIRST)
+        interleave_vector(z, SECOND)
+        tanh_scale(z - 2)
+        tanh_scale(z - 1)
+        exp_scale(z - 2)
+        exp_scale(z - 1)
+        store_y(z - 3, nc.scalar.copy)
+        quantize_h4(z, SECOND)
+        log_scale_apart(z)
+        product(z - 2)
+        product(z - 1)
+        couple(z - 2)
+        couple(z - 1)
+        tanh_scale(z)
+        exp_scale(z)
+        sum_ls(z - 2)
+        sum_ls(z - 1)
+        turn_y(z - 2)
+        turn_y(z - 1, "acc")
+        product(z)
+        sum_ls(z)
+        store_y(z - 2, nc.scalar.copy)
+        couple(z)
+        store_y(z - 1, nc.scalar.copy)
+        store_log_det()
+        turn_y(z, "turn", slice(0, 1))
+        turn_y(z, "turn", slice(1, 2))
+        store_y(z, nc.vector.tensor_copy, slice(0, 1))
+        store_y(z, nc.scalar.copy, slice(1, 2))

@@ -22,20 +22,27 @@ P = 128
 PACK = 4
 PASSES = MID // (P * PACK)
 TILES = B // P
+CHUNK = 2
+CHUNKS = TILES // CHUNK
+N = CHUNK * P
 HALF = W // 2
 BANK = 512
-CHUNK_TILES = (2,) * 16
-ALL, FIRST, SECOND = slice(0, PASSES), slice(0, 1), slice(1, 2)
+PAIRS = MID // P // 2
+ALL, FIRST, SECOND = slice(0, 2), slice(0, 1), slice(1, 2)
+
 BANK_BUFS = {"turn": 2, "acc": 3, "v": 1, "y": 1}
-X2_AT = (0, 256, 768)
+SUM_AT = BANK // 2
+X2_AT = (0, N, 3 * N)
+STAGES = 3
+LOAD_TILES = 4
+X_LOAD_CHUNKS = 4
+MX_ALIGN = 256
 
 
 def tile_affinecoupling_pa_t_w4_kernel(
     tc, h3_bytes, h3_scale, w4_words, w4_scales, b4, w5_words, w5_scales, b5, x, log_det_j, out_0, out_1
 ):
     nc = tc.nc
-    chunks = len(CHUNK_TILES)
-    first = [sum(CHUNK_TILES[:c]) for c in range(chunks)]
 
     with ExitStack() as ctx:
         keep = ctx.enter_context(tc.tile_pool(name="keep", bufs=1))
@@ -59,21 +66,20 @@ def tile_affinecoupling_pa_t_w4_kernel(
         nc.vector.memset(w4s_raw[:].bitcast(I32), 0)
         nc.vector.memset(w5s_raw[:].bitcast(I32), 0)
 
-        h3b = {}
-        xs = {}
+        h3_tile = {}
+        x_chunk = {}
 
         def load_h3(j0, tiles):
-            h3_group = keep.tile([P, tiles, MID], U8, name="h3b%d" % j0)
+            h3_group = keep.tile([P, tiles, MID], U8, name="h3_bytes%d" % j0)
             nc.sync.dma_start(out=h3_group[:], in_=h3_rows[:, j0 : j0 + tiles, :])
             for j in range(tiles):
-                h3b[j0 + j] = h3_group[:, j, :]
+                h3_tile[j0 + j] = h3_group[:, j, :]
 
-        def load_x(c0, count):
-            tiles = sum(CHUNK_TILES[c0 : c0 + count])
-            x_group = keep.tile([P, tiles, W], BF16, name="x%d" % c0)
-            nc.sync.dma_start(out=x_group[:], in_=x_rows[:, first[c0] : first[c0] + tiles, :])
-            for c in range(c0, c0 + count):
-                xs[c] = x_group[:, first[c] - first[c0] : first[c] - first[c0] + CHUNK_TILES[c], :]
+        def load_x(c0):
+            x_group = keep.tile([P, X_LOAD_CHUNKS * CHUNK, W], BF16, name="x%d" % c0)
+            nc.sync.dma_start(out=x_group[:], in_=x_rows[:, CHUNK * c0 : CHUNK * (c0 + X_LOAD_CHUNKS), :])
+            for i in range(X_LOAD_CHUNKS):
+                x_chunk[c0 + i] = x_group[:, CHUNK * i : CHUNK * (i + 1), :]
 
         def load_scale_rows(plane, scales):
             for q in range(4):
@@ -81,6 +87,11 @@ def tile_affinecoupling_pa_t_w4_kernel(
                     out=plane[32 * q : 32 * q + 4].bitcast(I32),
                     in_=scales[:, 4 * q : 4 * q + 4, :].rearrange("g r n -> r g n").bitcast(I32),
                 )
+
+        def load_words(words, name):
+            raw = keep.tile([P, PASSES, words.shape[2]], U8, name=name)
+            nc.sync.dma_start(out=raw[:].bitcast(I32), in_=words.rearrange("g p n -> p g n").bitcast(I32))
+            return raw
 
         b5_raw = keep.tile([P, 2], BF16, name="b5_raw")
         nc.sync.dma_start(out=b5_raw[:], in_=b5.rearrange("(p c) -> p c", p=P))
@@ -90,158 +101,128 @@ def tile_affinecoupling_pa_t_w4_kernel(
         load_h3(1, 1)
         scale_cols = keep.tile([P, PASSES, PACK], F32, name="scale_cols")
         nc.sync.dma_start(out=scale_cols[:], in_=h3_scale.rearrange("o (g p t) -> p (o g) t", p=P, t=PACK))
-        w4w_raw = keep.tile([P, PASSES, 2 * MID], U8, name="w4w_raw")
-        nc.sync.dma_start(out=w4w_raw[:].bitcast(I32), in_=w4_words.rearrange("g p n -> p g n").bitcast(I32))
-        load_h3(2, 2)
+        w4w_raw = load_words(w4_words, "w4w_raw")
+        load_h3(CHUNK, CHUNK)
         load_scale_rows(w4s_raw, w4_scales)
-        load_h3(4, 4)
+        load_h3(LOAD_TILES, LOAD_TILES)
         b4_cols = keep.tile([P, PASSES * PACK], BF16, name="b4_cols")
-        nc.sync.dma_start(out=b4_cols[:].rearrange("p (g t) -> p g t", t=PACK), in_=b4.rearrange("(g p t) -> p g t", p=P, t=PACK))
+        nc.sync.dma_start(
+            out=b4_cols[:].rearrange("p (g t) -> p g t", t=PACK), in_=b4.rearrange("(g p t) -> p g t", p=P, t=PACK)
+        )
         load_scale_rows(w5s_raw, w5_scales)
-        w5w_raw = keep.tile([P, PASSES, 2 * W], U8, name="w5w_raw")
-        nc.sync.dma_start(out=w5w_raw[:].bitcast(I32), in_=w5_words.rearrange("g p n -> p g n").bitcast(I32))
-        load_h3(8, 4)
-        ldj = keep.tile([P, TILES], BF16, name="ldj")
-        nc.sync.dma_start(out=ldj[:], in_=log_det_j.rearrange("(p j) -> p j", p=P))
-        load_x(0, 4)
-        for j0 in range(12, TILES, 4):
-            load_h3(j0, 4)
-        for c0 in range(4, chunks, 4):
-            load_x(c0, min(4, chunks - c0))
+        w5w_raw = load_words(w5_words, "w5w_raw")
+        load_h3(2 * LOAD_TILES, LOAD_TILES)
+        log_det_in = keep.tile([P, TILES], BF16, name="log_det_in")
+        nc.sync.dma_start(out=log_det_in[:], in_=log_det_j.rearrange("(p j) -> p j", p=P))
+        load_x(0)
+        for j0 in range(3 * LOAD_TILES, TILES, LOAD_TILES):
+            load_h3(j0, LOAD_TILES)
+        for c0 in range(X_LOAD_CHUNKS, CHUNKS, X_LOAD_CHUNKS):
+            load_x(c0)
 
-        w4w = keep.tile([P, PASSES, 2 * MID], U8, name="w4w", align_bytes=256)
-        w4s = keep.tile([P, PASSES, MID], U8, name="w4s", align_bytes=256)
-        w5w = keep.tile([P, PASSES, 2 * W], U8, name="w5w", align_bytes=256)
-        w5s = keep.tile([P, PASSES, W], U8, name="w5s", align_bytes=256)
+        w4w = keep.tile([P, PASSES, 2 * MID], U8, name="w4w", align_bytes=MX_ALIGN)
+        w4s = keep.tile([P, PASSES, MID], U8, name="w4s", align_bytes=MX_ALIGN)
+        w5w = keep.tile([P, PASSES, 2 * W], U8, name="w5w", align_bytes=MX_ALIGN)
+        w5s = keep.tile([P, PASSES, W], U8, name="w5s", align_bytes=MX_ALIGN)
 
-        def order_w4_words(a):
-            cols = slice(MID // 2 * a, MID // 2 * (a + 1))
-            nc.scalar.copy(
-                out=w4w[:].bitcast(U16)[:, :, cols].rearrange("p g (t m) -> p g t m", t=PACK),
-                in_=w4w_raw[:].bitcast(U16)[:, :, cols].rearrange("p g (m t) -> p g t m", t=PACK),
+        def reorder(copy, ordered, raw, groups):
+            copy(
+                out=ordered.rearrange("p g (t m) -> p g t m", t=groups),
+                in_=raw.rearrange("p g (m t) -> p g t m", t=groups),
             )
 
-        def order_w4_scales(a):
-            cols = slice(MID // 2 * a, MID // 2 * (a + 1))
-            nc.vector.tensor_copy(
-                out=w4s[:, :, cols].rearrange("p g (t m) -> p g t m", t=PACK),
-                in_=w4s_raw[:, :, cols].rearrange("p g (m t) -> p g t m", t=PACK),
-            )
+        def order_w4_words(half):
+            cols = slice(MID // 2 * half, MID // 2 * (half + 1))
+            reorder(nc.scalar.copy, w4w[:].bitcast(U16)[:, :, cols], w4w_raw[:].bitcast(U16)[:, :, cols], PACK)
 
-        def order_w5_words():
-            nc.scalar.copy(
-                out=w5w[:].bitcast(U16).rearrange("p g (c m) -> p g c m", c=2),
-                in_=w5w_raw[:].bitcast(U16).rearrange("p g (m c) -> p g c m", c=2),
-            )
+        def order_w4_scales(half):
+            cols = slice(MID // 2 * half, MID // 2 * (half + 1))
+            reorder(nc.vector.tensor_copy, w4s[:, :, cols], w4s_raw[:, :, cols], PACK)
 
-        def order_w5_scales():
-            nc.vector.tensor_copy(
-                out=w5s[:].rearrange("p g (c m) -> p g c m", c=2),
-                in_=w5s_raw[:].rearrange("p g (m c) -> p g c m", c=2),
-            )
-
-        log_det = keep.tile([P, TILES], F32, name="log_det")
-
-        wide = {}
-        turned = {}
-        turn_bank = {}
-        y_bank = {}
-        h3q = {}
-        h4_planes = {}
-        h4_rows = {}
-        h4q = {}
-        ls = {}
-        scale_e = {}
+        wide, turn_bank, h3_rows_k, h3q = {}, {}, {}, {}
+        h4_planes, h4_rows_k, h4q = {}, {}, {}
+        v_even, v_odd, ls, exp_ls, scaled_x2, y2 = {}, {}, {}, {}, {}, {}
+        y_bank, y_tile = {}, {}
         side = psum.tile([P, BANK], F32, name="side")
-        v_even = {}
-        v_odd = {}
-        prod = {}
-        y2t = {}
 
-        def live(c, j=0):
-            return 0 <= c < chunks and j < CHUNK_TILES[c]
+        def bank(shape, tag, name):
+            return psum.tile(shape, F32, tag=tag, bufs=BANK_BUFS[tag], name=name)
+
+        def stage(slot, name):
+            return work.tile([P, PASSES, N * PACK], BF16, tag="stage%d" % (slot % STAGES), bufs=1, name=name, align_bytes=MX_ALIGN)
 
         def widen(c, j):
-            if not live(c, j):
-                return
-            wide[c, j] = work.tile([P, MID], BF16, tag="wide", bufs=4, name="wide")
+            wide[c, j] = work.tile([P, MID], BF16, tag="wide", bufs=2 * CHUNK, name="wide")
             nc.scalar.copy(
                 out=wide[c, j][:].rearrange("p (u q e) -> p u q e", u=2, e=2),
-                in_=h3b[first[c] + j].bitcast(FP8).rearrange("p (q u e) -> p u q e", u=2, e=2),
+                in_=h3_tile[CHUNK * c + j].bitcast(FP8).rearrange("p (q u e) -> p u q e", u=2, e=2),
             )
 
-        def turn(c, j):
-            if not live(c, j):
-                return
-            words = wide[c, j][:].bitcast(F32)
-            turn_bank[c, j] = psum.tile([P, 2, PASSES, P], F32, tag="turn", bufs=2, name="turn")
-            for u in range(2):
-                for g in range(PASSES):
-                    at = (PASSES * u + g) * P
-                    nc.tensor.transpose(turn_bank[c, j][:, u, g, :], words[:, at : at + P], ident_f32[:])
+        def turn(c):
+            for j in range(CHUNK):
+                words = wide[c, j][:].bitcast(F32)
+                turn_bank[c, j] = bank([P, 2, PASSES, P], "turn", "turn")
+                for u in range(2):
+                    for g in range(PASSES):
+                        at = (PASSES * u + g) * P
+                        nc.tensor.transpose(turn_bank[c, j][:, u, g, :], words[:, at : at + P], ident_f32[:])
 
         def apply_scale(c, j):
-            if not live(c, j):
-                return
             if j == 0:
-                n = CHUNK_TILES[c] * P
-                turned[c] = work.tile([P, PASSES, n * PACK], BF16, tag="turned", name="turned", align_bytes=256)
+                h3_rows_k[c] = stage(c, "h3_rows_k")
             nc.vector.tensor_tensor(
-                out=turned[c][:, :, PACK * P * j : PACK * P * (j + 1)].rearrange("p g (r u e) -> p g r u e", u=2, e=2),
+                out=h3_rows_k[c][:, :, PACK * P * j : PACK * P * (j + 1)].rearrange("p g (r u e) -> p g r u e", u=2, e=2),
                 in0=turn_bank[c, j][:].bitcast(BF16).rearrange("p u g (r e) -> p g r u e", e=2),
                 in1=scale_cols[:].rearrange("p g (u e) -> p g u e", e=2).unsqueeze(2).to_broadcast([P, PASSES, P, 2, 2]),
                 op=ALU.mult,
             )
 
-        def quantize(store, c, source, tag, passes):
-            n = CHUNK_TILES[c] * P
+        def quantize(made, c, source, tag, passes):
             if passes.start == 0:
-                codes = work.tile([P, PASSES, n], U32, tag=tag + "_codes", bufs=3, name=tag + "_codes", align_bytes=256)
-                scales = work.tile([P, PASSES, n], U8, tag=tag + "_scales", bufs=3, name=tag + "_scales", align_bytes=256)
-                store[c] = codes, scales
+                codes = work.tile([P, PASSES, N], U32, tag=tag + "_codes", bufs=3, name=tag + "_codes", align_bytes=MX_ALIGN)
+                scales = work.tile([P, PASSES, N], U8, tag=tag + "_scales", bufs=3, name=tag + "_scales", align_bytes=MX_ALIGN)
+                made[c] = codes, scales
             nc.vector.quantize_mx(
-                out=store[c][0][:, passes, :].rearrange("p g n -> p (g n)").bitcast(FP8X4),
-                scales=store[c][1][:, passes, :].rearrange("p g n -> p (g n)"),
+                out=made[c][0][:, passes, :].rearrange("p g n -> p (g n)").bitcast(FP8X4),
+                scales=made[c][1][:, passes, :].rearrange("p g n -> p (g n)"),
                 in_=source[:, passes, :].rearrange("p g n -> p (g n)"),
             )
 
         def quantize_h3(c):
-            if live(c):
-                quantize(h3q, c, turned[c], "h3q", ALL)
+            quantize(h3q, c, h3_rows_k[c], "h3q", ALL)
 
-        def mx_product(acc, words, scales, col, operand, c):
+        def quantize_h4(c, passes):
+            quantize(h4q, c, h4_rows_k[c], "h4q", passes)
+
+        def mx_product(acc, words, scales, col, operand):
             for g in range(PASSES):
                 nc.tensor.matmul_mx(
                     out=acc,
                     lhsT=words[:, g, 2 * P * col : 2 * P * (col + 1)].bitcast(FP4X4),
                     lhsT_scale=scales[:, g, P * col : P * (col + 1)],
-                    rhs=operand[c][0][:, g, :].bitcast(FP8X4),
-                    rhs_scale=operand[c][1][:, g, :],
+                    rhs=operand[0][:, g, :].bitcast(FP8X4),
+                    rhs_scale=operand[1][:, g, :],
                     start=(g == 0),
                     stop=(g == PASSES - 1),
                 )
 
-        def hidden(c, pair):
-            if not live(c):
-                return
-            n = CHUNK_TILES[c] * P
-            if pair == 0:
-                h4_planes[c] = work.tile([P, PASSES * PACK, n], BF16, tag="h4_planes", name="h4_planes")
-            acc = psum.tile([P, 2, n], F32, tag="acc", bufs=3, name="acc")
-            for i in range(2):
-                mx_product(acc[:, i, :], w4w, w4s, 2 * pair + i, h3q, c)
-            for i in range(2):
-                col = 2 * pair + i
-                nc.scalar.activation(out=h4_planes[c][:, col, :], in_=acc[:, i, :], func=ACT.Relu, bias=b4_cols[:, col : col + 1])
+        def hidden(c):
+            h4_planes[c] = work.tile([P, PASSES * PACK, N], BF16, tag="h4_planes", name="h4_planes")
+            for pair in range(PAIRS):
+                acc = bank([P, 2, N], "acc", "acc")
+                for i in range(2):
+                    mx_product(acc[:, i, :], w4w, w4s, 2 * pair + i, h3q[c])
+                for i in range(2):
+                    col = 2 * pair + i
+                    nc.scalar.activation(
+                        out=h4_planes[c][:, col, :], in_=acc[:, i, :], func=ACT.Relu, bias=b4_cols[:, col : col + 1]
+                    )
 
-        def new_rows(c, tag):
-            n = CHUNK_TILES[c] * P
-            h4_rows[c] = work.tile([P, PASSES, n * PACK], BF16, tag=tag, bufs=1, name="h4_rows", align_bytes=256)
-
-        def interleave_gpsimd(c, passes):
+        def interleave_gpsimd(c):
+            h4_rows_k[c] = stage(c + 1, "h4_rows_k")
             nc.gpsimd.tensor_scalar(
-                out=h4_rows[c][:, passes, :].rearrange("p g (r t) -> p g r t", t=PACK),
-                in0=h4_planes[c][:].rearrange("p (g t) r -> p g r t", t=PACK)[:, passes],
+                out=h4_rows_k[c][:].rearrange("p g (r t) -> p g r t", t=PACK),
+                in0=h4_planes[c][:].rearrange("p (g t) r -> p g r t", t=PACK),
                 scalar1=1.0,
                 scalar2=0.0,
                 op0=ALU.mult,
@@ -249,109 +230,87 @@ def tile_affinecoupling_pa_t_w4_kernel(
             )
 
         def interleave_vector(c, passes):
+            if passes.start == 0:
+                h4_rows_k[c] = stage(c + 1, "h4_rows_k")
             nc.vector.tensor_copy(
-                out=h4_rows[c][:, passes, :].rearrange("p g (r i t) -> p g r t i", i=4, t=PACK),
+                out=h4_rows_k[c][:, passes, :].rearrange("p g (r i t) -> p g r t i", i=4, t=PACK),
                 in_=h4_planes[c][:].rearrange("p (g t) (r i) -> p g r t i", i=4, t=PACK)[:, passes],
             )
 
-        def quantize_h4(c, passes):
-            if live(c):
-                quantize(h4q, c, h4_rows[c], "h4q", passes)
+        def coupling_products(c, even, odd):
+            v_even[c], v_odd[c] = even, odd
+            mx_product(even, w5w, w5s, 0, h4q[c])
+            mx_product(odd, w5w, w5s, 1, h4q[c])
 
-        def log_scale(c, tag="v"):
-            if not live(c):
-                return
-            n = CHUNK_TILES[c] * P
-            bank = psum.tile([P, 2, n], F32, tag=tag, bufs=BANK_BUFS[tag], name="v")
-            v_even[c], v_odd[c] = bank[:, 0, :], bank[:, 1, :]
-            mx_product(v_even[c], w5w, w5s, 0, h4q, c)
-            mx_product(v_odd[c], w5w, w5s, 1, h4q, c)
+        def coupling_products_in(c, tag):
+            both = bank([P, 2, N], tag, "v")
+            coupling_products(c, both[:, 0, :], both[:, 1, :])
 
-        def log_scale_apart(c):
-            n = CHUNK_TILES[c] * P
-            even_bank = psum.tile([P, n], F32, tag="v", bufs=BANK_BUFS["v"], name="v_even")
-            odd_bank = psum.tile([P, n], F32, tag="acc", bufs=BANK_BUFS["acc"], name="v_odd")
-            v_even[c], v_odd[c] = even_bank[:], odd_bank[:]
-            mx_product(v_even[c], w5w, w5s, 0, h4q, c)
-            mx_product(v_odd[c], w5w, w5s, 1, h4q, c)
-
-        def tanh_scale(c):
-            if not live(c):
-                return
-            ls[c] = work.tile([P, CHUNK_TILES[c] * P], F32, tag="ls", bufs=3, name="ls")
+        def tanh(c):
+            ls[c] = work.tile([P, N], F32, tag="ls", bufs=4, name="ls")
             nc.scalar.activation(out=ls[c][:], in_=v_even[c], func=ACT.Tanh, bias=b5_cols[:, 0:1])
 
-        def exp_scale(c):
-            if not live(c):
-                return
-            scale_e[c] = work.tile([P, CHUNK_TILES[c] * P], F32, tag="scale_e", name="scale_e")
-            nc.scalar.activation(out=scale_e[c][:], in_=ls[c][:], func=ACT.Exp)
+        def exp(c):
+            exp_ls[c] = work.tile([P, N], F32, tag="exp_ls", name="exp_ls")
+            nc.scalar.activation(out=exp_ls[c][:], in_=ls[c][:], func=ACT.Exp)
+
+        def turned_x2(c):
+            at = X2_AT[c % len(X2_AT)]
+            return side[:].bitcast(BF16)[:, at : at + N]
 
         def turn_x2(c):
-            if not live(c):
-                return
-            for j in range(CHUNK_TILES[c]):
-                at = X2_AT[c % 3] + P * j
-                nc.tensor.transpose(side[:].bitcast(BF16)[:, at : at + P], xs[c][:, j, 1::2], ident_bf16[:])
+            for j in range(CHUNK):
+                nc.tensor.transpose(turned_x2(c)[:, P * j : P * (j + 1)], x_chunk[c][:, j, 1::2], ident_bf16[:])
 
         def sum_ls(c):
-            if not live(c):
-                return
-            for j in range(CHUNK_TILES[c]):
-                at = BANK // 2 + first[c] + j
+            for j in range(CHUNK):
+                at = SUM_AT + CHUNK * c + j
                 nc.tensor.matmul(side[:, at : at + 1], lhsT=ls[c][:, P * j : P * (j + 1)], rhs=ones[:], start=True, stop=True)
 
         def product(c):
-            if not live(c):
-                return
-            n = CHUNK_TILES[c] * P
-            prod[c] = work.tile([P, n], F32, tag="prod", name="prod")
-            nc.vector.tensor_tensor(out=prod[c][:], in0=side[:].bitcast(BF16)[:, X2_AT[c % 3] : X2_AT[c % 3] + n], in1=scale_e[c][:], op=ALU.mult)
+            scaled_x2[c] = work.tile([P, N], F32, tag="scaled_x2", name="scaled_x2")
+            nc.vector.tensor_tensor(out=scaled_x2[c][:], in0=turned_x2(c), in1=exp_ls[c][:], op=ALU.mult)
 
         def couple(c):
-            if not live(c):
-                return
-            y2t[c] = work.tile([P, CHUNK_TILES[c] * P], F32, tag="y2t", name="y2t")
+            y2[c] = work.tile([P, N], F32, tag="y2", bufs=3, name="y2")
             nc.vector.scalar_tensor_tensor(
-                out=y2t[c][:], in0=v_odd[c], scalar=b5_cols[:, 1:2], in1=prod[c][:], op0=ALU.add, op1=ALU.add
+                out=y2[c][:], in0=v_odd[c], scalar=b5_cols[:, 1:2], in1=scaled_x2[c][:], op0=ALU.add, op1=ALU.add
             )
 
-        def turn_y(c, tag="y", part=slice(0, 2)):
-            if not live(c):
-                return
-            tiles = part.stop - part.start
-            bank = psum.tile([P, 2, tiles * HALF], F32, tag=tag, bufs=BANK_BUFS[tag], name="y_bank")
-            y_bank[c, part.start] = bank
+        def turn_y(c, tag, tiles=ALL):
+            count = tiles.stop - tiles.start
+            planes = bank([P, 2, count * HALF], tag, "y_bank")
+            y_bank[c, tiles.start] = planes
+            for j in range(count):
+                at = P * (tiles.start + j)
+                nc.tensor.transpose(planes[:, 1, HALF * j : HALF * (j + 1)], y2[c][:, at : at + P], ident_f32[:])
             nc.tensor.matmul(
-                bank[:, 0, :],
+                planes[:, 0, :],
                 lhsT=ident_bf16[:],
-                rhs=xs[c][:, part, :].rearrange("p j w -> p (j w)")[:, 0::2],
+                rhs=x_chunk[c][:, tiles, :].rearrange("p j w -> p (j w)")[:, 0::2],
                 start=True,
                 stop=True,
             )
-            for j in range(tiles):
-                at = P * (part.start + j)
-                nc.tensor.transpose(bank[:, 1, HALF * j : HALF * (j + 1)], y2t[c][:, at : at + P], ident_f32[:])
+            y_tile[c, tiles.start] = work.tile([P, count, W], F32, tag="y", bufs=5, name="y")
 
-        def store_y(c, copy_out, part=slice(0, 2)):
-            if not live(c):
-                return
-            tiles = part.stop - part.start
-            y = work.tile([P, tiles, W], F32, tag="y", bufs=5, name="y")
-            copy_out(
-                out=y[:].rearrange("p j (m c) -> p (j m) c", c=2),
-                in_=y_bank[c, part.start][:].rearrange("p c n -> p n c"),
+        def copy_y(copy, c, first=0, pairs=slice(None)):
+            copy(
+                out=y_tile[c, first][:].rearrange("p j (m e) -> p (j m) e", e=2)[:, pairs, :],
+                in_=y_bank[c, first][:].rearrange("p e n -> p n e")[:, pairs, :],
             )
-            nc.sync.dma_start(out=y_rows[:, first[c] + part.start : first[c] + part.stop, :], in_=y[:])
 
-        def store_log_det():
-            nc.vector.tensor_tensor(out=log_det[:], in0=side[:, BANK // 2 : BANK // 2 + TILES], in1=ldj[:], op=ALU.add)
-            nc.sync.dma_start(out=out_1.rearrange("(p j) -> p j", p=P), in_=log_det[:])
+        def store_y(c, tiles=ALL):
+            nc.sync.dma_start(
+                out=y_rows[:, CHUNK * c + tiles.start : CHUNK * c + tiles.stop, :], in_=y_tile[c, tiles.start][:]
+            )
+
+        def finish_y(copy, c, tiles=ALL):
+            copy_y(copy, c, tiles.start)
+            store_y(c, tiles)
 
         widen(0, 0)
         widen(0, 1)
-        turn(0, 0)
-        turn(0, 1)
+        turn(0)
         order_w4_words(0)
         widen(1, 0)
         widen(1, 1)
@@ -361,94 +320,108 @@ def tile_affinecoupling_pa_t_w4_kernel(
         quantize_h3(0)
         order_w4_scales(1)
         order_w4_words(1)
-        turn(1, 0)
-        turn(1, 1)
+        turn(1)
         widen(2, 0)
         widen(2, 1)
-        for step in range(chunks - 2):
-            apply_scale(step + 1, 0)
-            product(step - 3)
-            store_y(step - 4, nc.vector.tensor_copy)
-            couple(step - 3)
-            apply_scale(step + 1, 1)
-            if step == 0:
-                order_w5_scales()
-            for pair in range(4):
-                hidden(step, pair)
-            log_scale(step - 2)
-            tanh_scale(step - 2)
-            quantize_h4(step - 1, ALL)
-            quantize_h3(step + 1)
-            new_rows(step, "rows")
-            interleave_gpsimd(step, ALL)
-            turn(step + 2, 0)
-            turn(step + 2, 1)
-            turn_x2(step - 2)
-            sum_ls(step - 3)
-            turn_y(step - 3)
-            widen(step + 3, 0)
-            exp_scale(step - 2)
-            widen(step + 3, 1)
-            if step == 1:
-                order_w5_words()
-        z = chunks - 1
+
+        for s in range(CHUNKS - 2):
+            if s >= 3:
+                product(s - 3)
+            apply_scale(s + 1, 0)
+            if s >= 3:
+                couple(s - 3)
+            if s >= 4:
+                copy_y(nc.scalar.copy, s - 4, pairs=slice(0, HALF))
+            apply_scale(s + 1, 1)
+            if s >= 4:
+                copy_y(nc.vector.tensor_copy, s - 4, pairs=slice(HALF, 2 * HALF))
+                store_y(s - 4)
+            if s == 0:
+                reorder(nc.vector.tensor_copy, w5s[:], w5s_raw[:], 2)
+            hidden(s)
+            if s >= 2:
+                coupling_products_in(s - 2, "v")
+                tanh(s - 2)
+            quantize_h3(s + 1)
+            if s >= 1:
+                quantize_h4(s - 1, ALL)
+            interleave_gpsimd(s)
+            if s >= 3:
+                sum_ls(s - 3)
+            turn(s + 2)
+            if s >= 2:
+                turn_x2(s - 2)
+            if s >= 3:
+                turn_y(s - 3, "y")
+            if s + 3 < CHUNKS:
+                widen(s + 3, 0)
+            if s >= 2:
+                exp(s - 2)
+            if s + 3 < CHUNKS:
+                widen(s + 3, 1)
+            if s == 1:
+                reorder(nc.scalar.copy, w5w[:].bitcast(U16), w5w_raw[:].bitcast(U16), 2)
+
+        z = CHUNKS - 1
+        turn_x2(z - 3)
         apply_scale(z, 0)
         product(z - 4)
-        store_y(z - 5, nc.scalar.copy)
+        finish_y(nc.scalar.copy, z - 5)
         apply_scale(z, 1)
         couple(z - 4)
-        for pair in range(4):
-            hidden(z - 1, pair)
-        log_scale(z - 3)
-        tanh_scale(z - 3)
+        hidden(z - 1)
+        coupling_products_in(z - 3, "v")
+        tanh(z - 3)
         quantize_h3(z)
         quantize_h4(z - 2, ALL)
-        turn_x2(z - 3)
-        sum_ls(z - 4)
-        turn_y(z - 4)
-        exp_scale(z - 3)
-        store_y(z - 4, nc.scalar.copy)
-        new_rows(z - 1, "rows_a")
+        exp(z - 3)
         interleave_vector(z - 1, ALL)
-        for pair in range(4):
-            hidden(z, pair)
+
+        hidden(z)
         product(z - 3)
         quantize_h4(z - 1, ALL)
-        couple(z - 3)
-        new_rows(z, "rows_b")
         interleave_vector(z, FIRST)
-        log_scale(z - 2, "turn")
-        log_scale(z - 1, "turn")
+        couple(z - 3)
+        coupling_products_in(z - 2, "turn")
+        coupling_products_in(z - 1, "turn")
+        sum_ls(z - 4)
+        sum_ls(z - 3)
         for c in range(z - 2, z + 1):
             turn_x2(c)
-        sum_ls(z - 3)
-        turn_y(z - 3)
+        turn_y(z - 4, "y")
         quantize_h4(z, FIRST)
         interleave_vector(z, SECOND)
-        tanh_scale(z - 2)
-        tanh_scale(z - 1)
-        exp_scale(z - 2)
-        exp_scale(z - 1)
-        store_y(z - 3, nc.scalar.copy)
+        for emit in (tanh, exp):
+            emit(z - 2)
+            emit(z - 1)
+        finish_y(nc.scalar.copy, z - 4)
         quantize_h4(z, SECOND)
-        log_scale_apart(z)
-        product(z - 2)
-        product(z - 1)
-        couple(z - 2)
-        couple(z - 1)
-        tanh_scale(z)
-        exp_scale(z)
+
+        last_even = bank([P, N], "v", "last_even")
+        last_odd = bank([P, N], "acc", "last_odd")
+        coupling_products(z, last_even[:], last_odd[:])
+        for emit in (product, couple):
+            emit(z - 2)
+            emit(z - 1)
+        tanh(z)
+        exp(z)
+        turn_y(z - 3, "acc")
         sum_ls(z - 2)
         sum_ls(z - 1)
-        turn_y(z - 2)
+        turn_y(z - 2, "y")
         turn_y(z - 1, "acc")
+        finish_y(nc.vector.tensor_copy, z - 3)
         product(z)
         sum_ls(z)
-        store_y(z - 2, nc.scalar.copy)
+        finish_y(nc.scalar.copy, z - 2)
         couple(z)
-        store_y(z - 1, nc.scalar.copy)
-        store_log_det()
-        turn_y(z, "turn", slice(0, 1))
-        turn_y(z, "turn", slice(1, 2))
-        store_y(z, nc.vector.tensor_copy, slice(0, 1))
-        store_y(z, nc.scalar.copy, slice(1, 2))
+        finish_y(nc.scalar.copy, z - 1)
+
+        log_det = keep.tile([P, TILES], F32, name="log_det")
+        nc.vector.tensor_tensor(out=log_det[:], in0=side[:, SUM_AT : SUM_AT + TILES], in1=log_det_in[:], op=ALU.add)
+        nc.sync.dma_start(out=out_1.rearrange("(p j) -> p j", p=P), in_=log_det[:])
+
+        turn_y(z, "turn", FIRST)
+        turn_y(z, "turn", SECOND)
+        finish_y(nc.vector.tensor_copy, z, FIRST)
+        finish_y(nc.scalar.copy, z, SECOND)

from contextlib import ExitStack

import concourse.mybir as mybir
from concourse.masks import make_identity

B, MID, W = 4096, 1024, 256
FLOPS = 2 * B * MID * (MID + W)

F32 = mybir.dt.float32
BF16 = mybir.dt.bfloat16
I32 = mybir.dt.int32
U32 = mybir.dt.uint32
U16 = mybir.dt.uint16
U8 = mybir.dt.uint8
FP8 = mybir.dt.float8_e4m3fn
FP8X4 = mybir.dt.float8_e4m3fn_x4
FP4X4 = mybir.dt.float4_e2m1fn_x4
ALU = mybir.AluOpType
ACT = mybir.ActivationFunctionType

P = 128
PACK = 4
PASSES = MID // (P * PACK)
TILES = B // P
CHUNK = 2
CHUNKS = TILES // CHUNK
N = CHUNK * P
HALF = W // 2
BANK = 512
PAIRS = MID // P // 2
ALL, FIRST, SECOND = slice(0, 2), slice(0, 1), slice(1, 2)

BANK_BUFS = {"turn": 2, "acc": 3, "v": 1, "y": 1}
SUM_AT = BANK // 2
X2_AT = (0, N, 3 * N)
STAGES = 3
LOAD_TILES = 4
X_LOAD_CHUNKS = 4
MX_ALIGN = 256


def tile_affinecoupling_pa_t_w4_kernel(
    tc, h3_bytes, h3_scale, w4_words, w4_scales, b4, w5_words, w5_scales, b5, x, log_det_j, out_0, out_1
):
    nc = tc.nc

    with ExitStack() as ctx:
        keep = ctx.enter_context(tc.tile_pool(name="keep", bufs=1))
        work = ctx.enter_context(tc.tile_pool(name="work", bufs=2))
        psum = ctx.enter_context(tc.psum_pool(name="psum", bufs=1))
        ctx.enter_context(tc.manual_schedule())

        h3_rows = h3_bytes.rearrange("(p j) k -> p j k", p=P)
        x_rows = x.rearrange("(p j) w -> p j w", p=P)
        y_rows = out_0.rearrange("(p j) w -> p j w", p=P)

        ident_f32 = keep.tile([P, P], F32, name="ident_f32")
        make_identity(nc, ident_f32[:])
        ident_bf16 = keep.tile([P, P], BF16, name="ident_bf16")
        make_identity(nc, ident_bf16[:])
        ones = keep.tile([P, 1], F32, name="ones")
        nc.gpsimd.memset(ones[:], 1.0)

        w4s_raw = keep.tile([P, PASSES, MID], U8, name="w4s_raw")
        w5s_raw = keep.tile([P, PASSES, W], U8, name="w5s_raw")
        nc.vector.memset(w4s_raw[:].bitcast(I32), 0)
        nc.vector.memset(w5s_raw[:].bitcast(I32), 0)

        h3_tile = {}
        x_chunk = {}

        def load_h3(j0, tiles):
            h3_group = keep.tile([P, tiles, MID], U8, name="h3_bytes%d" % j0)
            nc.sync.dma_start(out=h3_group[:], in_=h3_rows[:, j0 : j0 + tiles, :])
            for j in range(tiles):
                h3_tile[j0 + j] = h3_group[:, j, :]

        def load_x(c0):
            x_group = keep.tile([P, X_LOAD_CHUNKS * CHUNK, W], BF16, name="x%d" % c0)
            nc.sync.dma_start(out=x_group[:], in_=x_rows[:, CHUNK * c0 : CHUNK * (c0 + X_LOAD_CHUNKS), :])
            for i in range(X_LOAD_CHUNKS):
                x_chunk[c0 + i] = x_group[:, CHUNK * i : CHUNK * (i + 1), :]

        def load_scale_rows(plane, scales):
            for q in range(4):
                nc.sync.dma_start(
                    out=plane[32 * q : 32 * q + 4].bitcast(I32),
                    in_=scales[:, 4 * q : 4 * q + 4, :].rearrange("g r n -> r g n").bitcast(I32),
                )

        def load_words(words, name):
            raw = keep.tile([P, PASSES, words.shape[2]], U8, name=name)
            nc.sync.dma_start(out=raw[:].bitcast(I32), in_=words.rearrange("g p n -> p g n").bitcast(I32))
            return raw

        b5_raw = keep.tile([P, 2], BF16, name="b5_raw")
        nc.sync.dma_start(out=b5_raw[:], in_=b5.rearrange("(p c) -> p c", p=P))
        b5_cols = keep.tile([P, 2], F32, name="b5_cols")
        nc.scalar.activation(out=b5_cols[:], in_=b5_raw[:], func=ACT.Copy)
        load_h3(0, 1)
        load_h3(1, 1)
        scale_cols = keep.tile([P, PASSES, PACK], F32, name="scale_cols")
        nc.sync.dma_start(out=scale_cols[:], in_=h3_scale.rearrange("o (g p t) -> p (o g) t", p=P, t=PACK))
        w4w_raw = load_words(w4_words, "w4w_raw")
        load_h3(CHUNK, CHUNK)
        load_scale_rows(w4s_raw, w4_scales)
        load_h3(LOAD_TILES, LOAD_TILES)
        b4_cols = keep.tile([P, PASSES * PACK], BF16, name="b4_cols")
        nc.sync.dma_start(
            out=b4_cols[:].rearrange("p (g t) -> p g t", t=PACK), in_=b4.rearrange("(g p t) -> p g t", p=P, t=PACK)
        )
        load_scale_rows(w5s_raw, w5_scales)
        w5w_raw = load_words(w5_words, "w5w_raw")
        load_h3(2 * LOAD_TILES, LOAD_TILES)
        log_det_in = keep.tile([P, TILES], BF16, name="log_det_in")
        nc.sync.dma_start(out=log_det_in[:], in_=log_det_j.rearrange("(p j) -> p j", p=P))
        load_x(0)
        for j0 in range(3 * LOAD_TILES, TILES, LOAD_TILES):
            load_h3(j0, LOAD_TILES)
        for c0 in range(X_LOAD_CHUNKS, CHUNKS, X_LOAD_CHUNKS):
            load_x(c0)

        w4w = keep.tile([P, PASSES, 2 * MID], U8, name="w4w", align_bytes=MX_ALIGN)
        w4s = keep.tile([P, PASSES, MID], U8, name="w4s", align_bytes=MX_ALIGN)
        w5w = keep.tile([P, PASSES, 2 * W], U8, name="w5w", align_bytes=MX_ALIGN)
        w5s = keep.tile([P, PASSES, W], U8, name="w5s", align_bytes=MX_ALIGN)

        def reorder(copy, ordered, raw, groups):
            copy(
                out=ordered.rearrange("p g (t m) -> p g t m", t=groups),
                in_=raw.rearrange("p g (m t) -> p g t m", t=groups),
            )

        def order_w4_words(half):
            cols = slice(MID // 2 * half, MID // 2 * (half + 1))
            reorder(nc.scalar.copy, w4w[:].bitcast(U16)[:, :, cols], w4w_raw[:].bitcast(U16)[:, :, cols], PACK)

        def order_w4_scales(half):
            cols = slice(MID // 2 * half, MID // 2 * (half + 1))
            reorder(nc.vector.tensor_copy, w4s[:, :, cols], w4s_raw[:, :, cols], PACK)

        wide, turn_bank, h3_rows_k, h3q = {}, {}, {}, {}
        h4_planes, h4_rows_k, h4q = {}, {}, {}
        v_even, v_odd, ls, exp_ls, scaled_x2, y2 = {}, {}, {}, {}, {}, {}
        y_bank, y_tile = {}, {}
        side = psum.tile([P, BANK], F32, name="side")

        def bank(shape, tag, name):
            return psum.tile(shape, F32, tag=tag, bufs=BANK_BUFS[tag], name=name)

        def stage(slot, name):
            return work.tile([P, PASSES, N * PACK], BF16, tag="stage%d" % (slot % STAGES), bufs=1, name=name, align_bytes=MX_ALIGN)

        def widen(c, j):
            wide[c, j] = work.tile([P, MID], BF16, tag="wide", bufs=2 * CHUNK, name="wide")
            nc.scalar.copy(
                out=wide[c, j][:].rearrange("p (u q e) -> p u q e", u=2, e=2),
                in_=h3_tile[CHUNK * c + j].bitcast(FP8).rearrange("p (q u e) -> p u q e", u=2, e=2),
            )

        def turn(c):
            for j in range(CHUNK):
                words = wide[c, j][:].bitcast(F32)
                turn_bank[c, j] = bank([P, 2, PASSES, P], "turn", "turn")
                for u in range(2):
                    for g in range(PASSES):
                        at = (PASSES * u + g) * P
                        nc.tensor.transpose(turn_bank[c, j][:, u, g, :], words[:, at : at + P], ident_f32[:])

        def apply_scale(c, j):
            if j == 0:
                h3_rows_k[c] = stage(c, "h3_rows_k")
            nc.vector.tensor_tensor(
                out=h3_rows_k[c][:, :, PACK * P * j : PACK * P * (j + 1)].rearrange("p g (r u e) -> p g r u e", u=2, e=2),
                in0=turn_bank[c, j][:].bitcast(BF16).rearrange("p u g (r e) -> p g r u e", e=2),
                in1=scale_cols[:].rearrange("p g (u e) -> p g u e", e=2).unsqueeze(2).to_broadcast([P, PASSES, P, 2, 2]),
                op=ALU.mult,
            )

        def quantize(made, c, source, tag, passes):
            if passes.start == 0:
                codes = work.tile([P, PASSES, N], U32, tag=tag + "_codes", bufs=3, name=tag + "_codes", align_bytes=MX_ALIGN)
                scales = work.tile([P, PASSES, N], U8, tag=tag + "_scales", bufs=3, name=tag + "_scales", align_bytes=MX_ALIGN)
                made[c] = codes, scales
            nc.vector.quantize_mx(
                out=made[c][0][:, passes, :].rearrange("p g n -> p (g n)").bitcast(FP8X4),
                scales=made[c][1][:, passes, :].rearrange("p g n -> p (g n)"),
                in_=source[:, passes, :].rearrange("p g n -> p (g n)"),
            )

        def quantize_h3(c):
            quantize(h3q, c, h3_rows_k[c], "h3q", ALL)

        def quantize_h4(c, passes):
            quantize(h4q, c, h4_rows_k[c], "h4q", passes)

        def mx_product(acc, words, scales, col, operand):
            for g in range(PASSES):
                nc.tensor.matmul_mx(
                    out=acc,
                    lhsT=words[:, g, 2 * P * col : 2 * P * (col + 1)].bitcast(FP4X4),
                    lhsT_scale=scales[:, g, P * col : P * (col + 1)],
                    rhs=operand[0][:, g, :].bitcast(FP8X4),
                    rhs_scale=operand[1][:, g, :],
                    start=(g == 0),
                    stop=(g == PASSES - 1),
                )

        def hidden(c):
            h4_planes[c] = work.tile([P, PASSES * PACK, N], BF16, tag="h4_planes", name="h4_planes")
            for pair in range(PAIRS):
                acc = bank([P, 2, N], "acc", "acc")
                for i in range(2):
                    mx_product(acc[:, i, :], w4w, w4s, 2 * pair + i, h3q[c])
                for i in range(2):
                    col = 2 * pair + i
                    nc.scalar.activation(
                        out=h4_planes[c][:, col, :], in_=acc[:, i, :], func=ACT.Relu, bias=b4_cols[:, col : col + 1]
                    )

        def interleave_gpsimd(c):
            h4_rows_k[c] = stage(c + 1, "h4_rows_k")
            nc.gpsimd.tensor_scalar(
                out=h4_rows_k[c][:].rearrange("p g (r t) -> p g r t", t=PACK),
                in0=h4_planes[c][:].rearrange("p (g t) r -> p g r t", t=PACK),
                scalar1=1.0,
                scalar2=0.0,
                op0=ALU.mult,
                op1=ALU.add,
            )

        def interleave_vector(c, passes):
            if passes.start == 0:
                h4_rows_k[c] = stage(c + 1, "h4_rows_k")
            nc.vector.tensor_copy(
                out=h4_rows_k[c][:, passes, :].rearrange("p g (r i t) -> p g r t i", i=4, t=PACK),
                in_=h4_planes[c][:].rearrange("p (g t) (r i) -> p g r t i", i=4, t=PACK)[:, passes],
            )

        def coupling_products(c, even, odd):
            v_even[c], v_odd[c] = even, odd
            mx_product(even, w5w, w5s, 0, h4q[c])
            mx_product(odd, w5w, w5s, 1, h4q[c])

        def coupling_products_in(c, tag):
            both = bank([P, 2, N], tag, "v")
            coupling_products(c, both[:, 0, :], both[:, 1, :])

        def tanh(c):
            ls[c] = work.tile([P, N], F32, tag="ls", bufs=4, name="ls")
            nc.scalar.activation(out=ls[c][:], in_=v_even[c], func=ACT.Tanh, bias=b5_cols[:, 0:1])

        def exp(c):
            exp_ls[c] = work.tile([P, N], F32, tag="exp_ls", name="exp_ls")
            nc.scalar.activation(out=exp_ls[c][:], in_=ls[c][:], func=ACT.Exp)

        def turned_x2(c):
            at = X2_AT[c % len(X2_AT)]
            return side[:].bitcast(BF16)[:, at : at + N]

        def turn_x2(c):
            for j in range(CHUNK):
                nc.tensor.transpose(turned_x2(c)[:, P * j : P * (j + 1)], x_chunk[c][:, j, 1::2], ident_bf16[:])

        def sum_ls(c):
            for j in range(CHUNK):
                at = SUM_AT + CHUNK * c + j
                nc.tensor.matmul(side[:, at : at + 1], lhsT=ls[c][:, P * j : P * (j + 1)], rhs=ones[:], start=True, stop=True)

        def product(c):
            scaled_x2[c] = work.tile([P, N], F32, tag="scaled_x2", name="scaled_x2")
            nc.vector.tensor_tensor(out=scaled_x2[c][:], in0=turned_x2(c), in1=exp_ls[c][:], op=ALU.mult)

        def couple(c):
            y2[c] = work.tile([P, N], F32, tag="y2", bufs=3, name="y2")
            nc.vector.scalar_tensor_tensor(
                out=y2[c][:], in0=v_odd[c], scalar=b5_cols[:, 1:2], in1=scaled_x2[c][:], op0=ALU.add, op1=ALU.add
            )

        def turn_y(c, tag, tiles=ALL):
            count = tiles.stop - tiles.start
            planes = bank([P, 2, count * HALF], tag, "y_bank")
            y_bank[c, tiles.start] = planes
            for j in range(count):
                at = P * (tiles.start + j)
                nc.tensor.transpose(planes[:, 1, HALF * j : HALF * (j + 1)], y2[c][:, at : at + P], ident_f32[:])
            nc.tensor.matmul(
                planes[:, 0, :],
                lhsT=ident_bf16[:],
                rhs=x_chunk[c][:, tiles, :].rearrange("p j w -> p (j w)")[:, 0::2],
                start=True,
                stop=True,
            )
            y_tile[c, tiles.start] = work.tile([P, count, W], F32, tag="y", bufs=5, name="y")

        def copy_y(copy, c, first=0, pairs=slice(None)):
            copy(
                out=y_tile[c, first][:].rearrange("p j (m e) -> p (j m) e", e=2)[:, pairs, :],
                in_=y_bank[c, first][:].rearrange("p e n -> p n e")[:, pairs, :],
            )

        def store_y(c, tiles=ALL):
            nc.sync.dma_start(
                out=y_rows[:, CHUNK * c + tiles.start : CHUNK * c + tiles.stop, :], in_=y_tile[c, tiles.start][:]
            )

        def finish_y(copy, c, tiles=ALL):
            copy_y(copy, c, tiles.start)
            store_y(c, tiles)

        widen(0, 0)
        widen(0, 1)
        turn(0)
        order_w4_words(0)
        widen(1, 0)
        widen(1, 1)
        apply_scale(0, 0)
        apply_scale(0, 1)
        order_w4_scales(0)
        quantize_h3(0)
        order_w4_scales(1)
        order_w4_words(1)
        turn(1)
        widen(2, 0)
        widen(2, 1)

        for s in range(CHUNKS - 2):
            if s >= 3:
                product(s - 3)
            apply_scale(s + 1, 0)
            if s >= 3:
                couple(s - 3)
            if s >= 4:
                copy_y(nc.scalar.copy, s - 4, pairs=slice(0, HALF))
            apply_scale(s + 1, 1)
            if s >= 4:
                copy_y(nc.vector.tensor_copy, s - 4, pairs=slice(HALF, 2 * HALF))
                store_y(s - 4)
            if s == 0:
                reorder(nc.vector.tensor_copy, w5s[:], w5s_raw[:], 2)
            hidden(s)
            if s >= 2:
                coupling_products_in(s - 2, "v")
                tanh(s - 2)
            quantize_h3(s + 1)
            if s >= 1:
                quantize_h4(s - 1, ALL)
            interleave_gpsimd(s)
            if s >= 3:
                sum_ls(s - 3)
            turn(s + 2)
            if s >= 2:
                turn_x2(s - 2)
            if s >= 3:
                turn_y(s - 3, "y")
            if s + 3 < CHUNKS:
                widen(s + 3, 0)
            if s >= 2:
                exp(s - 2)
            if s + 3 < CHUNKS:
                widen(s + 3, 1)
            if s == 1:
                reorder(nc.scalar.copy, w5w[:].bitcast(U16), w5w_raw[:].bitcast(U16), 2)

        z = CHUNKS - 1
        turn_x2(z - 3)
        apply_scale(z, 0)
        product(z - 4)
        finish_y(nc.scalar.copy, z - 5)
        apply_scale(z, 1)
        couple(z - 4)
        hidden(z - 1)
        coupling_products_in(z - 3, "v")
        tanh(z - 3)
        quantize_h3(z)
        quantize_h4(z - 2, ALL)
        exp(z - 3)
        interleave_vector(z - 1, ALL)

        hidden(z)
        product(z - 3)
        quantize_h4(z - 1, ALL)
        interleave_vector(z, FIRST)
        couple(z - 3)
        coupling_products_in(z - 2, "turn")
        coupling_products_in(z - 1, "turn")
        sum_ls(z - 4)
        sum_ls(z - 3)
        for c in range(z - 2, z + 1):
            turn_x2(c)
        turn_y(z - 4, "y")
        quantize_h4(z, FIRST)
        interleave_vector(z, SECOND)
        for emit in (tanh, exp):
            emit(z - 2)
            emit(z - 1)
        finish_y(nc.scalar.copy, z - 4)
        quantize_h4(z, SECOND)

        last_even = bank([P, N], "v", "last_even")
        last_odd = bank([P, N], "acc", "last_odd")
        coupling_products(z, last_even[:], last_odd[:])
        for emit in (product, couple):
            emit(z - 2)
            emit(z - 1)
        tanh(z)
        exp(z)
        turn_y(z - 3, "acc")
        sum_ls(z - 2)
        sum_ls(z - 1)
        turn_y(z - 2, "y")
        turn_y(z - 1, "acc")
        finish_y(nc.vector.tensor_copy, z - 3)
        product(z)
        sum_ls(z)
        finish_y(nc.scalar.copy, z - 2)
        couple(z)
        finish_y(nc.scalar.copy, z - 1)

        log_det = keep.tile([P, TILES], F32, name="log_det")
        nc.vector.tensor_tensor(out=log_det[:], in0=side[:, SUM_AT : SUM_AT + TILES], in1=log_det_in[:], op=ALU.add)
        nc.sync.dma_start(out=out_1.rearrange("(p j) -> p j", p=P), in_=log_det[:])

        turn_y(z, "turn", FIRST)
        turn_y(z, "turn", SECOND)
        finish_y(nc.vector.tensor_copy, z, FIRST)
        finish_y(nc.scalar.copy, z, SECOND)
